import numpy as np
import ml_dtypes


def mxq(x, axis, fmt="e4m3"):
    dtype, down = {"e4m3": (ml_dtypes.float8_e4m3fn, 7), "e5m2": (ml_dtypes.float8_e5m2, 14)}[fmt]
    v = np.moveaxis(np.asarray(x, np.float32).astype(ml_dtypes.bfloat16).astype(np.float64), axis, -1)
    blocks = v.reshape(v.shape[:-1] + (-1, 32))
    amax = np.abs(blocks).max(-1, keepdims=True)
    byte = np.maximum(np.where(amax > 0, np.frexp(amax)[1] - 1 + 127, 0) - down, 1)
    scale = np.exp2(byte - 127.0)
    codes = (blocks / scale).astype(np.float32).astype(dtype).astype(np.float64)
    return np.moveaxis((codes * scale).reshape(v.shape), -1, axis)


WIDE = False


def mx_kscale(k):
    if not WIDE:
        return np.ones(k)
    levels = np.array([10, -10, 5, -5, 0])
    a = np.random.permutation(np.resize(levels, k // 512 * 4)).reshape(k // 512, 4)
    idx = np.arange(k)
    return np.exp2(a[idx // 512, idx % 128 // 32])


BF16 = ml_dtypes.bfloat16


def bf(x):
    return np.asarray(x, np.float32).astype(BF16)


def f64(x):
    return np.asarray(x).astype(np.float64)


B, S, NH, HD, DO, QB = 2, 1024, 8, 128, 1024, 512
H = NH * HD
NEG = -1e9


def alibi_slopes(n):
    p = 1
    while p * 2 <= n:
        p *= 2
    base = 2.0 ** (-(2.0 ** (-(np.log2(p) - 3.0))))
    slopes = base ** np.arange(1, 1 + p, dtype=np.float64)
    if p != n:
        extra = 2.0 ** (-(2.0 ** (-(np.log2(2 * p) - 3.0))))
        r = min(p, n - p)
        slopes = np.concatenate([slopes, extra ** np.arange(1, 1 + 2 * r, 2, dtype=np.float64)])
    return slopes


def column_offsets(n):
    return np.sign(np.random.standard_normal(n)) * (1.0 + 0.5 * np.random.random(n))


def setup_inputs():
    t = mx_kscale(H)
    mu = column_offsets(H)
    return {"q": bf(np.random.standard_normal((B, NH, S, HD))),
            "k": bf(np.random.standard_normal((B, NH, S, HD))),
            "v": bf((mu.reshape(NH, 1, HD) + np.random.standard_normal((B, NH, S, HD)) * 0.6) * t.reshape(NH, 1, HD)),
            "w_out": bf(np.random.standard_normal((H, DO)) / np.sqrt(H) / t[:, None]),
            "b_out": bf(np.random.standard_normal(DO) * 0.3)}


def reference(q, k, v, w_out, b_out):
    q, k = f64(q), f64(k)
    vq = mxq(f64(v), 2, "e4m3")
    slopes = alibi_slopes(NH)
    pos = np.arange(S, dtype=np.float64)
    pieces = []
    for n in range(S // QB):
        lo, hi = n * QB, (n + 1) * QB
        s = q[:, :, lo:hi] @ k[:, :, :hi].transpose(0, 1, 3, 2) * HD ** (-0.5)
        rel = pos[None, :hi] - pos[lo:hi, None]
        s = s + slopes[:, None, None] * rel[None]
        causal = pos[None, :hi] <= pos[lo:hi, None]
        s = np.where(causal, s, NEG)
        e = np.exp(s - s.max(-1, keepdims=True))
        pieces.append((mxq(e, 3, "e4m3") @ vq[:, :, :hi]) / e.sum(-1, keepdims=True))
    ctx = np.concatenate(pieces, axis=2)
    ctx = ctx.transpose(0, 2, 1, 3).reshape(B, S, H)
    return (mxq(ctx, 2, "e4m3") @ mxq(f64(w_out), 0, "e4m3")) + f64(b_out)

@@ -1,0 +1,356 @@
+from contextlib import ExitStack
+
+import concourse.mybir as mybir
+from concourse.masks import make_identity
+
+BF16 = mybir.dt.bfloat16
+F32 = mybir.dt.float32
+I32 = mybir.dt.int32
+U32 = mybir.dt.uint32
+U8 = mybir.dt.uint8
+FP8X4 = mybir.dt.float8_e4m3fn_x4
+ALU = mybir.AluOpType
+ACT = mybir.ActivationFunctionType
+
+B, NH, S, HD, DO = 2, 8, 1024, 128, 1024
+H = NH * HD
+P = 128
+BANK = 512
+K_PASS = 512
+CHUNK = 256
+Q_BLOCKS = S // P
+HALF = Q_BLOCKS // 2
+SCALE = HD ** -0.5
+MASKED = 1.0e30
+
+FLOPS = 2 * 2 * B * NH * HD * (K_PASS * K_PASS + K_PASS * S) + 2 * B * S * H * DO
+
+
+HEADS = B * NH
+ITEMS = HEADS * Q_BLOCKS
+
+LOAD_LEAD = 2 * Q_BLOCKS
+V_REGROUP_LEAD = 6
+Q_TURN_LEAD = 4
+K_TURN_LEAD = 3
+V_QUANTISE_LEAD = 2
+W_STEP = 10
+PROJECT_LAG = 11
+
+
+def key_passes(block):
+    return block // HALF + 1
+
+
+def regroup(nc, rows, grouped):
+    nc.gpsimd.tensor_scalar(
+        out=grouped,
+        in0=rows.rearrange("p (g t) w -> p g w t", t=4),
+        scalar1=1.0,
+        scalar2=0.0,
+        op0=ALU.mult,
+        op1=ALU.add,
+    )
+
+
+def turn_words(nc, psum, pool, rows, n_pass, ident_f32, tag):
+    words = rows.bitcast(F32)
+    turned = psum.tile([P, 2 * n_pass, P], F32, tag="turn")
+    for piece in range(2 * n_pass):
+        nc.tensor.transpose(turned[:, piece, :], words[:, piece * P : (piece + 1) * P], ident_f32)
+    grouped = pool.tile([P, n_pass, P, 2], F32, tag=tag + "_grouped", align_bytes=64)
+    nc.scalar.copy(out=grouped[:], in_=turned[:].rearrange("p (g u) r -> p g r u", u=2))
+    return grouped
+
+
+def quantise_words(nc, pool, grouped, n_pass, tag):
+    codes = pool.tile([P, n_pass * P], U32, tag=tag + "_codes", align_bytes=64)
+    scales = pool.tile([P, n_pass * P], U8, tag=tag + "_scales", align_bytes=64)
+    nc.vector.quantize_mx(
+        out=codes[:].bitcast(FP8X4),
+        scales=scales[:],
+        in_=grouped[:].rearrange("p g r u -> p (g r u)").bitcast(BF16),
+    )
+    return codes, scales
+
+
+def tile_bloomattention_pa_kernel(tc, q, k, v, w_out, b_out, out):
+    nc = tc.nc
+    with ExitStack() as ctx:
+        const = ctx.enter_context(tc.tile_pool(name="const", bufs=1))
+        loads = ctx.enter_context(tc.tile_pool(name="loads", bufs=3))
+        heads = ctx.enter_context(tc.tile_pool(name="heads", bufs=2))
+        blocks = ctx.enter_context(tc.tile_pool(name="blocks", bufs=3))
+        turn_psum = ctx.enter_context(tc.psum_pool(name="turn_psum", bufs=2))
+        bank_psum = ctx.enter_context(tc.psum_pool(name="bank_psum", bufs=4))
+        context_psum = ctx.enter_context(tc.psum_pool(name="context_psum", bufs=2))
+
+        ident_bf = const.tile([P, P], BF16, name="ident_bf")
+        make_identity(nc, ident_bf[:])
+        ident_f32 = const.tile([P, P], F32, name="ident_f32")
+        make_identity(nc, ident_f32[:])
+
+        distance_int = const.tile([P, S], I32, name="distance_int")
+        nc.gpsimd.iota(distance_int[:], pattern=[[-1, S]], base=S - P, channel_multiplier=1)
+        distance = const.tile([P, S], F32, name="distance")
+        nc.vector.tensor_copy(out=distance[:], in_=distance_int[:])
+        nc.gpsimd.affine_select(
+            out=distance[:, S - P :],
+            in_=distance[:, S - P :],
+            pattern=[[-1, P]],
+            compare_op=ALU.is_ge,
+            fill=MASKED,
+            base=0,
+            channel_multiplier=1,
+        )
+        penalty = []
+        for h in range(NH):
+            strip = const.tile([P, S], F32, name="penalty%d" % h)
+            nc.vector.tensor_scalar(
+                out=strip[:], in0=distance[:], scalar1=2.0 ** -(h + 1), scalar2=None, op0=ALU.mult
+            )
+            penalty.append(strip)
+
+        e_sets = []
+        for copy in range(2):
+            e_tiles = []
+            for n in range(Q_BLOCKS):
+                e_tile = const.tile([P, K_PASS * key_passes(n)], BF16, name="e%d_%d" % (copy, n))
+                if P * (n + 1) < K_PASS * key_passes(n):
+                    nc.vector.memset(e_tile[:, P * (n + 1) :], 0.0)
+                e_tiles.append(e_tile)
+            e_sets.append(e_tiles)
+
+        w_rows = const.tile([P, H // P, DO], BF16, name="w_rows")
+        w_grouped = const.tile([P, H // K_PASS, DO, 4], BF16, name="w_grouped", align_bytes=64)
+        w_codes = const.tile([P, H // K_PASS, DO], U32, name="w_codes", align_bytes=64)
+        w_scales = const.tile([P, H // K_PASS, DO], U8, name="w_scales", align_bytes=64)
+        bias = const.tile([P, DO], BF16, name="bias")
+
+        q_rows, k_rows, v_rows, q_cols, k_cols = {}, {}, {}, {}, {}
+        v_grouped, v_codes, v_scales = {}, {}, {}
+        cost_min, row_sum, row_scale = {}, {}, {}
+        c_rows, context = {}, {}
+        score_banks, cost, e_grouped, e_codes, e_scales = {}, {}, {}, {}, {}
+        c_grouped, c_codes, c_scales = {}, {}, {}
+
+        def load_head(head):
+            b, h = divmod(head, NH)
+            q_tile = loads.tile([P, Q_BLOCKS, HD], BF16, tag="q_rows")
+            nc.sync.dma_start(out=q_tile[:], in_=q[b, h].rearrange("(n p) d -> p n d", p=P))
+            k_tile = loads.tile([P, Q_BLOCKS, HD], BF16, tag="k_rows")
+            nc.sync.dma_start(out=k_tile[:], in_=k[b, h].rearrange("(n p) d -> p n d", p=P))
+            v_tile = loads.tile([P, S // P, HD], BF16, tag="v_rows")
+            nc.sync.dma_start(
+                out=v_tile[:].rearrange("p (c e) d -> p c (e d)", e=2),
+                in_=v[b, h].rearrange("(c p e) d -> p c (e d)", p=P, e=2),
+            )
+            q_rows[head], k_rows[head], v_rows[head] = q_tile, k_tile, v_tile
+
+        def turn_rows(rows, tag):
+            turned = turn_psum.tile([P, S], BF16, tag="turn")
+            for n in range(Q_BLOCKS):
+                nc.tensor.transpose(turned[:, n * P : (n + 1) * P], rows[:, n, :], ident_bf[:])
+            columns = heads.tile([P, S], BF16, tag=tag)
+            nc.scalar.copy(out=columns[:], in_=turned[:])
+            return columns
+
+        def turn_q(head):
+            q_cols[head] = turn_rows(q_rows[head], "q_cols")
+
+        def turn_k(head):
+            k_cols[head] = turn_rows(k_rows[head], "k_cols")
+
+        def regroup_v(head):
+            grouped = heads.tile([P, S // K_PASS, HD, 4], BF16, tag="v_grouped", align_bytes=64)
+            regroup(nc, v_rows[head][:], grouped[:])
+            v_grouped[head] = grouped
+
+        def quantise_v(head):
+            codes = heads.tile([P, S // K_PASS, HD], U32, tag="v_codes", align_bytes=64)
+            scales = heads.tile([P, S // K_PASS, HD], U8, tag="v_scales", align_bytes=64)
+            nc.vector.quantize_mx(
+                out=codes[:].rearrange("p g d -> p (g d)").bitcast(FP8X4),
+                scales=scales[:].rearrange("p g d -> p (g d)"),
+                in_=v_grouped[head][:].rearrange("p g d t -> p (g d t)"),
+            )
+            v_codes[head], v_scales[head] = codes, scales
+
+        def scores(item):
+            head, n = divmod(item, Q_BLOCKS)
+            keys = P * (n + 1)
+            score_banks[item] = []
+            for k0 in range(0, keys, BANK):
+                width = min(BANK, keys - k0)
+                bank = bank_psum.tile([P, BANK], F32, tag="bank")
+                nc.tensor.matmul(
+                    out=bank[:, :width],
+                    lhsT=q_cols[head][:, n * P : (n + 1) * P],
+                    rhs=k_cols[head][:, k0 : k0 + width],
+                    start=True,
+                    stop=True,
+                )
+                score_banks[item].append(bank)
+
+        def costs(item):
+            head, n = divmod(item, Q_BLOCKS)
+            keys = P * (n + 1)
+            if n == 0:
+                lowest = heads.tile([P, Q_BLOCKS], F32, tag="cost_min")
+                sums = heads.tile([P, Q_BLOCKS], F32, tag="row_sum")
+                factors = heads.tile([P, Q_BLOCKS], F32, tag="row_scale")
+                cost_min[head], row_sum[head], row_scale[head] = lowest, sums, factors
+            t = blocks.tile([P, S], F32, tag="cost", bufs=4)
+            for k0 in range(0, keys, BANK):
+                width = min(BANK, keys - k0)
+                nc.vector.scalar_tensor_tensor(
+                    out=t[:, k0 : k0 + width],
+                    in0=score_banks[item][k0 // BANK][:, :width],
+                    scalar=-SCALE,
+                    in1=penalty[head % NH][:, S - keys + k0 : S - keys + k0 + width],
+                    op0=ALU.mult,
+                    op1=ALU.add,
+                )
+            cost[item] = t
+
+        def minima(item):
+            head, n = divmod(item, Q_BLOCKS)
+            nc.vector.tensor_reduce(
+                out=cost_min[head][:, n : n + 1],
+                in_=cost[item][:, : P * (n + 1)],
+                axis=mybir.AxisListType.X,
+                op=ALU.min,
+            )
+
+        def exponentials(item):
+            head, n = divmod(item, Q_BLOCKS)
+            keys = P * (n + 1)
+            nc.scalar.activation(
+                out=e_sets[head % 2][n][:, :keys],
+                in_=cost[item][:, :keys],
+                func=ACT.Exp,
+                bias=cost_min[head][:, n : n + 1],
+                scale=-1.0,
+                accum_out=row_sum[head][:, n : n + 1],
+            )
+
+        def turn_e(item):
+            head, n = divmod(item, Q_BLOCKS)
+            e_grouped[item] = turn_words(
+                nc, turn_psum, blocks, e_sets[head % 2][n][:], key_passes(n), ident_f32[:], "e"
+            )
+
+        def quantise_e(item):
+            head, n = divmod(item, Q_BLOCKS)
+            e_codes[item], e_scales[item] = quantise_words(nc, blocks, e_grouped[item], key_passes(n), "e")
+            if n % HALF == HALF - 1:
+                nc.vector.reciprocal(
+                    out=row_scale[head][:, n - (HALF - 1) : n + 1], in_=row_sum[head][:, n - (HALF - 1) : n + 1]
+                )
+
+        def contexts(item):
+            head, n = divmod(item, Q_BLOCKS)
+            if n % HALF == 0:
+                bank = context_psum.tile([P, HALF, HD], F32, tag="context")
+                context[item // HALF] = bank
+            for g in range(key_passes(n)):
+                nc.tensor.matmul_mx(
+                    out=context[item // HALF][:, n % HALF, :],
+                    lhsT=e_codes[item][:, g * P : (g + 1) * P].bitcast(FP8X4),
+                    lhsT_scale=e_scales[item][:, g * P : (g + 1) * P],
+                    rhs=v_codes[head][:, g, :].bitcast(FP8X4),
+                    rhs_scale=v_scales[head][:, g, :],
+                    start=(g == 0),
+                    stop=(g == key_passes(n) - 1),
+                )
+
+        def normalise(item):
+            head, n = divmod(item, Q_BLOCKS)
+            b, h = divmod(head, NH)
+            if n % HALF != HALF - 1:
+                return
+            if h == 0 and n == HALF - 1:
+                rows = heads.tile([P, Q_BLOCKS, H], BF16, tag="c_rows")
+                c_rows[b] = rows
+            for m in range(n - (HALF - 1), n + 1):
+                nc.scalar.activation(
+                    out=c_rows[b][:, m, h * HD : (h + 1) * HD],
+                    in_=context[item // HALF][:, m % HALF, :],
+                    func=ACT.Copy,
+                    scale=row_scale[head][:, m : m + 1],
+                )
+
+        def turn_c(item):
+            head, n = divmod(item, Q_BLOCKS)
+            if head % NH == NH - 1:
+                c_grouped[item] = turn_words(
+                    nc, turn_psum, blocks, c_rows[head // NH][:, n, :], H // K_PASS, ident_f32[:], "c"
+                )
+
+        def quantise_c(item):
+            if item // Q_BLOCKS % NH == NH - 1:
+                c_codes[item], c_scales[item] = quantise_words(nc, blocks, c_grouped[item], H // K_PASS, "c")
+
+        def project(item):
+            head, n = divmod(item, Q_BLOCKS)
+            if head % NH != NH - 1:
+                return
+            result = blocks.tile([P, DO], F32, tag="result")
+            for n0 in range(0, DO, BANK):
+                product = bank_psum.tile([P, BANK], F32, tag="bank")
+                for g in range(H // K_PASS):
+                    nc.tensor.matmul_mx(
+                        out=product[:],
+                        lhsT=c_codes[item][:, g * P : (g + 1) * P].bitcast(FP8X4),
+                        lhsT_scale=c_scales[item][:, g * P : (g + 1) * P],
+                        rhs=w_codes[:, g, n0 : n0 + BANK].bitcast(FP8X4),
+                        rhs_scale=w_scales[:, g, n0 : n0 + BANK],
+                        start=(g == 0),
+                        stop=(g == H // K_PASS - 1),
+                    )
+                nc.vector.tensor_tensor(
+                    out=result[:, n0 : n0 + BANK], in0=product[:], in1=bias[:, n0 : n0 + BANK], op=ALU.add
+                )
+            nc.sync.dma_start(out=out[head // NH, n * P : (n + 1) * P, :], in_=result[:])
+
+        def for_item(stage, item):
+            if 0 <= item < ITEMS:
+                stage(item)
+
+        def for_head(prepare, step):
+            if step % Q_BLOCKS == 0 and 0 <= step // Q_BLOCKS < HEADS:
+                prepare(step // Q_BLOCKS)
+
+        with tc.manual_schedule():
+            for step in range(-LOAD_LEAD, ITEMS + PROJECT_LAG + 3):
+                for_item(scores, step)
+                for_item(costs, step - 1)
+                for_item(minima, step - 2)
+                for_item(exponentials, step - 3)
+                for_item(turn_e, step - 4)
+                for_item(quantise_e, step - 5)
+                for_item(contexts, step - 6)
+                for_item(normalise, step - 7)
+                for_item(turn_c, step - PROJECT_LAG)
+                for_item(quantise_c, step - PROJECT_LAG - 1)
+                for_item(project, step - PROJECT_LAG - 2)
+                for_head(load_head, step + LOAD_LEAD)
+                for_head(regroup_v, step + V_REGROUP_LEAD)
+                for_head(turn_q, step + Q_TURN_LEAD)
+                for_head(turn_k, step + K_TURN_LEAD)
+                for_head(quantise_v, step + V_QUANTISE_LEAD)
+                if step == 0:
+                    nc.sync.dma_start(
+                        out=w_rows[:].rearrange("p (c e) n -> p c (e n)", e=2),
+                        in_=w_out.rearrange("(c p e) n -> p c (e n)", p=P, e=2),
+                    )
+                    nc.sync.dma_start(out=bias[:], in_=b_out.partition_broadcast(P))
+                for g in range(H // K_PASS):
+                    if step == W_STEP + 2 * g * Q_BLOCKS:
+                        regroup(nc, w_rows[:, 4 * g : 4 * g + 4, :], w_grouped[:, g : g + 1, :, :])
+                    if step == W_STEP + (2 * g + 1) * Q_BLOCKS:
+                        nc.vector.quantize_mx(
+                            out=w_codes[:, g, :].bitcast(FP8X4),
+                            scales=w_scales[:, g, :],
+                            in_=w_grouped[:, g, :, :].rearrange("p n t -> p (n t)"),
+                        )

@@ -11,20 +11,20 @@ U8 = mybir.dt.uint8
 FP8X4 = mybir.dt.float8_e4m3fn_x4
 ALU = mybir.AluOpType
 ACT = mybir.ActivationFunctionType
+ROW = mybir.AxisListType.X
 
 B, NH, S, HD, DO = 2, 8, 1024, 128, 1024
 H = NH * HD
 P = 128
 BANK = 512
 K_PASS = 512
-CHUNK = 256
 Q_BLOCKS = S // P
-HALF = Q_BLOCKS // 2
+HALF = K_PASS // P
 SCALE = HD ** -0.5
 MASKED = 1.0e30
+PIECES = 3
 
 FLOPS = 2 * 2 * B * NH * HD * (K_PASS * K_PASS + K_PASS * S) + 2 * B * S * H * DO
-
 
 HEADS = B * NH
 ITEMS = HEADS * Q_BLOCKS
@@ -38,10 +38,6 @@ W_STEP = 10
 PROJECT_LAG = 11
 
 
-def key_passes(block):
-    return block // HALF + 1
-
-
 def regroup(nc, rows, grouped):
     nc.gpsimd.tensor_scalar(
         out=grouped,
@@ -53,11 +49,15 @@ def regroup(nc, rows, grouped):
     )
 
 
-def turn_words(nc, psum, pool, rows, n_pass, ident_f32, tag):
+def turn_words(nc, psum, rows, n_pass, ident_f32):
     words = rows.bitcast(F32)
     turned = psum.tile([P, 2 * n_pass, P], F32, tag="turn")
     for piece in range(2 * n_pass):
         nc.tensor.transpose(turned[:, piece, :], words[:, piece * P : (piece + 1) * P], ident_f32)
+    return turned
+
+
+def gather_words(nc, pool, turned, n_pass, tag):
     grouped = pool.tile([P, n_pass, P, 2], F32, tag=tag + "_grouped", align_bytes=64)
     nc.scalar.copy(out=grouped[:], in_=turned[:].rearrange("p (g u) r -> p g r u", u=2))
     return grouped
@@ -81,8 +81,9 @@ def tile_bloomattention_pa_kernel(tc, q, k, v, w_out, b_out, out):
         loads = ctx.enter_context(tc.tile_pool(name="loads", bufs=3))
         heads = ctx.enter_context(tc.tile_pool(name="heads", bufs=2))
         blocks = ctx.enter_context(tc.tile_pool(name="blocks", bufs=3))
-        turn_psum = ctx.enter_context(tc.psum_pool(name="turn_psum", bufs=2))
-        bank_psum = ctx.enter_context(tc.psum_pool(name="bank_psum", bufs=4))
+        near_psum = ctx.enter_context(tc.psum_pool(name="near_psum", bufs=1))
+        far_psum = ctx.enter_context(tc.psum_pool(name="far_psum", bufs=2))
+        turn_psum = ctx.enter_context(tc.psum_pool(name="turn_psum", bufs=3))
         context_psum = ctx.enter_context(tc.psum_pool(name="context_psum", bufs=2))
 
         ident_bf = const.tile([P, P], BF16, name="ident_bf")
@@ -90,13 +91,13 @@ def tile_bloomattention_pa_kernel(tc, q, k, v, w_out, b_out, out):
         ident_f32 = const.tile([P, P], F32, name="ident_f32")
         make_identity(nc, ident_f32[:])
 
-        distance_int = const.tile([P, S], I32, name="distance_int")
-        nc.gpsimd.iota(distance_int[:], pattern=[[-1, S]], base=S - P, channel_multiplier=1)
-        distance = const.tile([P, S], F32, name="distance")
+        distance_int = const.tile([P, BANK], I32, name="distance_int")
+        nc.gpsimd.iota(distance_int[:], pattern=[[-1, BANK]], base=BANK - P, channel_multiplier=1)
+        distance = const.tile([P, BANK], F32, name="distance")
         nc.vector.tensor_copy(out=distance[:], in_=distance_int[:])
         nc.gpsimd.affine_select(
-            out=distance[:, S - P :],
-            in_=distance[:, S - P :],
+            out=distance[:, BANK - P :],
+            in_=distance[:, BANK - P :],
             pattern=[[-1, P]],
             compare_op=ALU.is_ge,
             fill=MASKED,
@@ -105,18 +106,77 @@ def tile_bloomattention_pa_kernel(tc, q, k, v, w_out, b_out, out):
         )
         penalty = []
         for h in range(NH):
-            strip = const.tile([P, S], F32, name="penalty%d" % h)
+            strip = const.tile([P, BANK], F32, name="penalty%d" % h)
             nc.vector.tensor_scalar(
                 out=strip[:], in0=distance[:], scalar1=2.0 ** -(h + 1), scalar2=None, op0=ALU.mult
             )
             penalty.append(strip)
 
+        root_left = const.tile([P, PIECES], F32, name="root_left")
+        root = const.tile([P, PIECES], BF16, name="root")
+        nc.vector.tensor_scalar(
+            out=root_left[:, 0:1], in0=ident_f32[:, 0:1], scalar1=0.0, scalar2=HD ** 0.5, op0=ALU.mult, op1=ALU.add
+        )
+        for r in range(PIECES):
+            nc.vector.tensor_copy(out=root[:, r : r + 1], in_=root_left[:, r : r + 1])
+            if r + 1 < PIECES:
+                nc.vector.tensor_tensor(
+                    out=root_left[:, r + 1 : r + 2],
+                    in0=root_left[:, r : r + 1],
+                    in1=root[:, r : r + 1],
+                    op=ALU.subtract,
+                )
+        block_start = const.tile([P, HALF], I32, name="block_start")
+        nc.gpsimd.iota(block_start[:], pattern=[[P, HALF]], base=0, channel_multiplier=0)
+        lane = const.tile([P, HALF], I32, name="lane")
+        nc.gpsimd.iota(lane[:], pattern=[[0, HALF]], base=0, channel_multiplier=1)
+        by_query = const.tile([P, HALF, P], BF16, name="by_query")
+        by_key = const.tile([P, HALF, P], BF16, name="by_key")
+        nc.vector.memset(by_query[:], 0.0)
+        nc.vector.memset(by_key[:], 0.0)
+        query_rows = by_query[:].rearrange("p b (r s) -> p b r s", s=4)
+        key_rows = by_key[:].rearrange("p b (r s) -> p b r s", s=4)
+        pieces = root[:].unsqueeze(1).unsqueeze(3).to_broadcast([P, HALF, PIECES, 2])
+        nc.vector.tensor_copy(out=query_rows[:, :, 0:PIECES, 0:2], in_=pieces)
+        nc.vector.tensor_copy(out=key_rows[:, :, 0:PIECES, 2:4], in_=pieces)
+        starts = block_start[:].unsqueeze(2).to_broadcast([P, HALF, PIECES])
+        lanes = lane[:].unsqueeze(2).to_broadcast([P, HALF, PIECES])
+        nc.vector.tensor_scalar(
+            out=key_rows[:, :, 0:PIECES, 0], in0=starts, scalar1=1.0, scalar2=float(P - BANK), op0=ALU.mult, op1=ALU.add
+        )
+        nc.vector.tensor_scalar(
+            out=key_rows[:, :, 0:PIECES, 1], in0=lanes, scalar1=1.0, scalar2=float(1 - P), op0=ALU.mult, op1=ALU.add
+        )
+        nc.vector.tensor_scalar(
+            out=query_rows[:, :, 0:PIECES, 2], in0=starts, scalar1=-1.0, scalar2=0.0, op0=ALU.mult, op1=ALU.add
+        )
+        nc.vector.tensor_scalar(
+            out=query_rows[:, :, 0:PIECES, 3], in0=lanes, scalar1=-1.0, scalar2=-1.0, op0=ALU.mult, op1=ALU.add
+        )
+        far_keys = const.tile([P, BANK], BF16, name="far_keys")
+        far_unit = const.tile([P, BANK], BF16, name="far_unit")
+        far_queries = []
+        for h in range(NH):
+            sloped = const.tile([P, BANK], BF16, name="far_queries%d" % h)
+            far_queries.append(sloped)
+
+        def turn_far_operands():
+            for by_position, by_row in ((by_key, far_keys), (by_query, far_unit)):
+                turned = turn_psum.tile([P, BANK], BF16, tag="turn")
+                for blk in range(HALF):
+                    nc.tensor.transpose(turned[:, blk * P : (blk + 1) * P], by_position[:, blk, :], ident_bf[:])
+                nc.vector.tensor_copy(out=by_row[:], in_=turned[:])
+            for h in range(NH):
+                nc.vector.tensor_scalar(
+                    out=far_queries[h][:], in0=far_unit[:], scalar1=2.0 ** -(h + 1), scalar2=None, op0=ALU.mult
+                )
+
         e_sets = []
         for copy in range(2):
             e_tiles = []
             for n in range(Q_BLOCKS):
-                e_tile = const.tile([P, K_PASS * key_passes(n)], BF16, name="e%d_%d" % (copy, n))
-                if P * (n + 1) < K_PASS * key_passes(n):
+                e_tile = const.tile([P, K_PASS * (n // HALF + 1)], BF16, name="e%d_%d" % (copy, n))
+                if (n + 1) % HALF != 0:
                     nc.vector.memset(e_tile[:, P * (n + 1) :], 0.0)
                 e_tiles.append(e_tile)
             e_sets.append(e_tiles)
@@ -129,10 +189,10 @@ def tile_bloomattention_pa_kernel(tc, q, k, v, w_out, b_out, out):
 
         q_rows, k_rows, v_rows, q_cols, k_cols = {}, {}, {}, {}, {}
         v_grouped, v_codes, v_scales = {}, {}, {}
-        cost_min, row_sum, row_scale = {}, {}, {}
+        cost_min, near_min, far_max, near_sum, far_sum, row_scale = {}, {}, {}, {}, {}, {}
         c_rows, context = {}, {}
-        score_banks, cost, e_grouped, e_codes, e_scales = {}, {}, {}, {}, {}
-        c_grouped, c_codes, c_scales = {}, {}, {}
+        near_bank, far_bank, cost, e_turned, e_grouped, e_codes, e_scales = {}, {}, {}, {}, {}, {}, {}
+        c_turned, c_grouped, c_codes, c_scales = {}, {}, {}, {}
 
         def load_head(head):
             b, h = divmod(head, NH)
@@ -176,84 +236,129 @@ def tile_bloomattention_pa_kernel(tc, q, k, v, w_out, b_out, out):
             )
             v_codes[head], v_scales[head] = codes, scales
 
-        def scores(item):
+        def near_scores(item):
             head, n = divmod(item, Q_BLOCKS)
-            keys = P * (n + 1)
-            score_banks[item] = []
-            for k0 in range(0, keys, BANK):
-                width = min(BANK, keys - k0)
-                bank = bank_psum.tile([P, BANK], F32, tag="bank")
-                nc.tensor.matmul(
-                    out=bank[:, :width],
-                    lhsT=q_cols[head][:, n * P : (n + 1) * P],
-                    rhs=k_cols[head][:, k0 : k0 + width],
-                    start=True,
-                    stop=True,
-                )
-                score_banks[item].append(bank)
+            near_0, near_n = n // HALF * BANK, (n % HALF + 1) * P
+            near = near_psum.tile([P, BANK], F32, tag="near")
+            nc.tensor.matmul(
+                out=near[:, :near_n],
+                lhsT=q_cols[head][:, n * P : (n + 1) * P],
+                rhs=k_cols[head][:, near_0 : near_0 + near_n],
+                start=True,
+                stop=True,
+            )
+            near_bank[item] = near
+
+        def far_scores(item):
+            head, n = divmod(item, Q_BLOCKS)
+            if n < HALF:
+                return
+            far = far_psum.tile([P, BANK], F32, tag="far")
+            nc.tensor.matmul(
+                out=far[:], lhsT=q_cols[head][:, n * P : (n + 1) * P], rhs=k_cols[head][:, :BANK], start=True, stop=False
+            )
+            nc.tensor.matmul(
+                out=far[:],
+                lhsT=far_queries[head % NH][:, (n - HALF) * P : (n - HALF + 1) * P],
+                rhs=far_keys[:],
+                start=False,
+                stop=True,
+            )
+            far_bank[item] = far
 
         def costs(item):
             head, n = divmod(item, Q_BLOCKS)
-            keys = P * (n + 1)
+            near_n = (n % HALF + 1) * P
             if n == 0:
                 lowest = heads.tile([P, Q_BLOCKS], F32, tag="cost_min")
-                sums = heads.tile([P, Q_BLOCKS], F32, tag="row_sum")
+                lowest_near = heads.tile([P, HALF], F32, tag="near_min")
+                highest_far = heads.tile([P, HALF], F32, tag="far_max")
+                sums_near = heads.tile([P, Q_BLOCKS], F32, tag="near_sum")
+                sums_far = heads.tile([P, HALF], F32, tag="far_sum")
                 factors = heads.tile([P, Q_BLOCKS], F32, tag="row_scale")
-                cost_min[head], row_sum[head], row_scale[head] = lowest, sums, factors
-            t = blocks.tile([P, S], F32, tag="cost", bufs=4)
-            for k0 in range(0, keys, BANK):
-                width = min(BANK, keys - k0)
-                nc.vector.scalar_tensor_tensor(
-                    out=t[:, k0 : k0 + width],
-                    in0=score_banks[item][k0 // BANK][:, :width],
-                    scalar=-SCALE,
-                    in1=penalty[head % NH][:, S - keys + k0 : S - keys + k0 + width],
-                    op0=ALU.mult,
-                    op1=ALU.add,
-                )
+                cost_min[head], near_min[head], far_max[head] = lowest, lowest_near, highest_far
+                near_sum[head], far_sum[head], row_scale[head] = sums_near, sums_far, factors
+            t = blocks.tile([P, BANK], F32, tag="cost", bufs=4)
+            nc.vector.scalar_tensor_tensor(
+                out=t[:, :near_n],
+                in0=near_bank[item][:, :near_n],
+                scalar=-SCALE,
+                in1=penalty[head % NH][:, BANK - near_n :],
+                op0=ALU.mult,
+                op1=ALU.add,
+            )
             cost[item] = t
 
         def minima(item):
             head, n = divmod(item, Q_BLOCKS)
-            nc.vector.tensor_reduce(
-                out=cost_min[head][:, n : n + 1],
-                in_=cost[item][:, : P * (n + 1)],
-                axis=mybir.AxisListType.X,
-                op=ALU.min,
-            )
+            near_n = (n % HALF + 1) * P
+            if n < HALF:
+                nc.vector.tensor_reduce(out=cost_min[head][:, n : n + 1], in_=cost[item][:, :near_n], axis=ROW, op=ALU.min)
+            else:
+                m = n - HALF
+                nc.vector.tensor_reduce(out=near_min[head][:, m : m + 1], in_=cost[item][:, :near_n], axis=ROW, op=ALU.min)
+                nc.vector.tensor_reduce(out=far_max[head][:, m : m + 1], in_=far_bank[item][:], axis=ROW, op=ALU.max)
+
+        def join_minima(item):
+            head, n = divmod(item, Q_BLOCKS)
+            if n >= HALF:
+                m = n - HALF
+                nc.vector.tensor_scalar(
+                    out=cost_min[head][:, n : n + 1],
+                    in0=far_max[head][:, m : m + 1],
+                    scalar1=-SCALE,
+                    scalar2=near_min[head][:, m : m + 1],
+                    op0=ALU.mult,
+                    op1=ALU.min,
+                )
 
         def exponentials(item):
             head, n = divmod(item, Q_BLOCKS)
-            keys = P * (n + 1)
+            near_0, near_n = n // HALF * BANK, (n % HALF + 1) * P
+            e_tile = e_sets[head % 2][n]
+            if n >= HALF:
+                nc.scalar.activation(
+                    out=e_tile[:, :BANK],
+                    in_=far_bank[item][:],
+                    func=ACT.Exp,
+                    bias=cost_min[head][:, n : n + 1],
+                    scale=SCALE,
+                    accum_out=far_sum[head][:, n - HALF : n - HALF + 1],
+                )
             nc.scalar.activation(
-                out=e_sets[head % 2][n][:, :keys],
-                in_=cost[item][:, :keys],
+                out=e_tile[:, near_0 : near_0 + near_n],
+                in_=cost[item][:, :near_n],
                 func=ACT.Exp,
                 bias=cost_min[head][:, n : n + 1],
                 scale=-1.0,
-                accum_out=row_sum[head][:, n : n + 1],
+                accum_out=near_sum[head][:, n : n + 1],
             )
 
         def turn_e(item):
             head, n = divmod(item, Q_BLOCKS)
-            e_grouped[item] = turn_words(
-                nc, turn_psum, blocks, e_sets[head % 2][n][:], key_passes(n), ident_f32[:], "e"
-            )
+            e_turned[item] = turn_words(nc, turn_psum, e_sets[head % 2][n][:], n // HALF + 1, ident_f32[:])
+
+        def gather_e(item):
+            e_grouped[item] = gather_words(nc, blocks, e_turned[item], item % Q_BLOCKS // HALF + 1, "e")
 
         def quantise_e(item):
             head, n = divmod(item, Q_BLOCKS)
-            e_codes[item], e_scales[item] = quantise_words(nc, blocks, e_grouped[item], key_passes(n), "e")
-            if n % HALF == HALF - 1:
-                nc.vector.reciprocal(
-                    out=row_scale[head][:, n - (HALF - 1) : n + 1], in_=row_sum[head][:, n - (HALF - 1) : n + 1]
+            if n == Q_BLOCKS - 1:
+                nc.vector.tensor_tensor(
+                    out=row_scale[head][:, HALF:], in0=near_sum[head][:, HALF:], in1=far_sum[head][:], op=ALU.add
                 )
+            e_codes[item], e_scales[item] = quantise_words(nc, blocks, e_grouped[item], n // HALF + 1, "e")
+            if n == HALF - 1:
+                nc.vector.reciprocal(out=row_scale[head][:, :HALF], in_=near_sum[head][:, :HALF])
+            if n == Q_BLOCKS - 1:
+                nc.vector.reciprocal(out=row_scale[head][:, HALF:], in_=row_scale[head][:, HALF:])
 
         def contexts(item):
             head, n = divmod(item, Q_BLOCKS)
             if n % HALF == 0:
                 bank = context_psum.tile([P, HALF, HD], F32, tag="context")
                 context[item // HALF] = bank
-            for g in range(key_passes(n)):
+            for g in range(n // HALF + 1):
                 nc.tensor.matmul_mx(
                     out=context[item // HALF][:, n % HALF, :],
                     lhsT=e_codes[item][:, g * P : (g + 1) * P].bitcast(FP8X4),
@@ -261,7 +366,7 @@ def tile_bloomattention_pa_kernel(tc, q, k, v, w_out, b_out, out):
                     rhs=v_codes[head][:, g, :].bitcast(FP8X4),
                     rhs_scale=v_scales[head][:, g, :],
                     start=(g == 0),
-                    stop=(g == key_passes(n) - 1),
+                    stop=(g == n // HALF),
                 )
 
         def normalise(item):
@@ -283,9 +388,8 @@ def tile_bloomattention_pa_kernel(tc, q, k, v, w_out, b_out, out):
         def turn_c(item):
             head, n = divmod(item, Q_BLOCKS)
             if head % NH == NH - 1:
-                c_grouped[item] = turn_words(
-                    nc, turn_psum, blocks, c_rows[head // NH][:, n, :], H // K_PASS, ident_f32[:], "c"
-                )
+                c_turned[item] = turn_words(nc, turn_psum, c_rows[head // NH][:, n, :], H // K_PASS, ident_f32[:])
+                c_grouped[item] = gather_words(nc, blocks, c_turned[item], H // K_PASS, "c")
 
         def quantise_c(item):
             if item // Q_BLOCKS % NH == NH - 1:
@@ -297,7 +401,7 @@ def tile_bloomattention_pa_kernel(tc, q, k, v, w_out, b_out, out):
                 return
             result = blocks.tile([P, DO], F32, tag="result")
             for n0 in range(0, DO, BANK):
-                product = bank_psum.tile([P, BANK], F32, tag="bank")
+                product = turn_psum.tile([P, BANK], F32, tag="turn")
                 for g in range(H // K_PASS):
                     nc.tensor.matmul_mx(
                         out=product[:],
@@ -323,13 +427,16 @@ def tile_bloomattention_pa_kernel(tc, q, k, v, w_out, b_out, out):
 
         with tc.manual_schedule():
             for step in range(-LOAD_LEAD, ITEMS + PROJECT_LAG + 3):
-                for_item(scores, step)
+                for_item(turn_e, step - 4)
+                for_item(contexts, step - 6)
+                for_item(near_scores, step)
+                for_item(far_scores, step - 1)
                 for_item(costs, step - 1)
                 for_item(minima, step - 2)
-                for_item(exponentials, step - 3)
-                for_item(turn_e, step - 4)
                 for_item(quantise_e, step - 5)
-                for_item(contexts, step - 6)
+                for_item(join_minima, step - 2)
+                for_item(exponentials, step - 3)
+                for_item(gather_e, step - 4)
                 for_item(normalise, step - 7)
                 for_item(turn_c, step - PROJECT_LAG)
                 for_item(quantise_c, step - PROJECT_LAG - 1)
@@ -339,6 +446,8 @@ def tile_bloomattention_pa_kernel(tc, q, k, v, w_out, b_out, out):
                 for_head(turn_q, step + Q_TURN_LEAD)
                 for_head(turn_k, step + K_TURN_LEAD)
                 for_head(quantise_v, step + V_QUANTISE_LEAD)
+                if step == -1:
+                    turn_far_operands()
                 if step == 0:
                     nc.sync.dma_start(
                         out=w_rows[:].rearrange("p (c e) n -> p c (e n)", e=2),

@@ -425,41 +425,40 @@ def tile_bloomattention_pa_kernel(tc, q, k, v, w_out, b_out, out):
             if step % Q_BLOCKS == 0 and 0 <= step // Q_BLOCKS < HEADS:
                 prepare(step // Q_BLOCKS)
 
-        with tc.manual_schedule():
-            for step in range(-LOAD_LEAD, ITEMS + PROJECT_LAG + 3):
-                for_item(turn_e, step - 4)
-                for_item(contexts, step - 6)
-                for_item(near_scores, step)
-                for_item(far_scores, step - 1)
-                for_item(costs, step - 1)
-                for_item(minima, step - 2)
-                for_item(quantise_e, step - 5)
-                for_item(join_minima, step - 2)
-                for_item(exponentials, step - 3)
-                for_item(gather_e, step - 4)
-                for_item(normalise, step - 7)
-                for_item(turn_c, step - PROJECT_LAG)
-                for_item(quantise_c, step - PROJECT_LAG - 1)
-                for_item(project, step - PROJECT_LAG - 2)
-                for_head(load_head, step + LOAD_LEAD)
-                for_head(regroup_v, step + V_REGROUP_LEAD)
-                for_head(turn_q, step + Q_TURN_LEAD)
-                for_head(turn_k, step + K_TURN_LEAD)
-                for_head(quantise_v, step + V_QUANTISE_LEAD)
-                if step == -1:
-                    turn_far_operands()
-                if step == 0:
-                    nc.sync.dma_start(
-                        out=w_rows[:].rearrange("p (c e) n -> p c (e n)", e=2),
-                        in_=w_out.rearrange("(c p e) n -> p c (e n)", p=P, e=2),
+        for step in range(-LOAD_LEAD, ITEMS + PROJECT_LAG + 3):
+            for_item(turn_e, step - 4)
+            for_item(contexts, step - 6)
+            for_item(near_scores, step)
+            for_item(far_scores, step - 1)
+            for_item(costs, step - 1)
+            for_item(minima, step - 2)
+            for_item(quantise_e, step - 5)
+            for_item(join_minima, step - 2)
+            for_item(exponentials, step - 3)
+            for_item(gather_e, step - 4)
+            for_item(normalise, step - 7)
+            for_item(turn_c, step - PROJECT_LAG)
+            for_item(quantise_c, step - PROJECT_LAG - 1)
+            for_item(project, step - PROJECT_LAG - 2)
+            for_head(load_head, step + LOAD_LEAD)
+            for_head(regroup_v, step + V_REGROUP_LEAD)
+            for_head(turn_q, step + Q_TURN_LEAD)
+            for_head(turn_k, step + K_TURN_LEAD)
+            for_head(quantise_v, step + V_QUANTISE_LEAD)
+            if step == -1:
+                turn_far_operands()
+            if step == 0:
+                nc.sync.dma_start(
+                    out=w_rows[:].rearrange("p (c e) n -> p c (e n)", e=2),
+                    in_=w_out.rearrange("(c p e) n -> p c (e n)", p=P, e=2),
+                )
+                nc.sync.dma_start(out=bias[:], in_=b_out.partition_broadcast(P))
+            for g in range(H // K_PASS):
+                if step == W_STEP + 2 * g * Q_BLOCKS:
+                    regroup(nc, w_rows[:, 4 * g : 4 * g + 4, :], w_grouped[:, g : g + 1, :, :])
+                if step == W_STEP + (2 * g + 1) * Q_BLOCKS:
+                    nc.vector.quantize_mx(
+                        out=w_codes[:, g, :].bitcast(FP8X4),
+                        scales=w_scales[:, g, :],
+                        in_=w_grouped[:, g, :, :].rearrange("p n t -> p (n t)"),
                     )
-                    nc.sync.dma_start(out=bias[:], in_=b_out.partition_broadcast(P))
-                for g in range(H // K_PASS):
-                    if step == W_STEP + 2 * g * Q_BLOCKS:
-                        regroup(nc, w_rows[:, 4 * g : 4 * g + 4, :], w_grouped[:, g : g + 1, :, :])
-                    if step == W_STEP + (2 * g + 1) * Q_BLOCKS:
-                        nc.vector.quantize_mx(
-                            out=w_codes[:, g, :].bitcast(FP8X4),
-                            scales=w_scales[:, g, :],
-                            in_=w_grouped[:, g, :, :].rearrange("p n t -> p (n t)"),
-                        )

@@ -22,20 +22,17 @@ Q_BLOCKS = S // P
 HALF = K_PASS // P
 SCALE = HD ** -0.5
 MASKED = 1.0e30
-PIECES = 3
 
 FLOPS = 2 * 2 * B * NH * HD * (K_PASS * K_PASS + K_PASS * S) + 2 * B * S * H * DO
 
 HEADS = B * NH
-ITEMS = HEADS * Q_BLOCKS
+UNITS = Q_BLOCKS // 2
 
-LOAD_LEAD = 2 * Q_BLOCKS
-V_REGROUP_LEAD = 6
-Q_TURN_LEAD = 4
-K_TURN_LEAD = 3
-V_QUANTISE_LEAD = 2
-W_STEP = 10
-PROJECT_LAG = 11
+LOAD_LEAD = 10
+W_STEP = 5
+PROJECT_LAG = 3
+TURNS = 3
+PROJECT_EVERY = 3
 
 
 def regroup(nc, rows, grouped):
@@ -49,23 +46,19 @@ def regroup(nc, rows, grouped):
     )
 
 
-def turn_words(nc, psum, rows, n_pass, ident_f32):
+def turn_words(nc, turned, rows, n_pass, ident_f32):
     words = rows.bitcast(F32)
-    turned = psum.tile([P, 2 * n_pass, P], F32, tag="turn")
     for piece in range(2 * n_pass):
         nc.tensor.transpose(turned[:, piece, :], words[:, piece * P : (piece + 1) * P], ident_f32)
-    return turned
 
 
-def gather_words(nc, pool, turned, n_pass, tag):
-    grouped = pool.tile([P, n_pass, P, 2], F32, tag=tag + "_grouped", align_bytes=64)
-    nc.scalar.copy(out=grouped[:], in_=turned[:].rearrange("p (g u) r -> p g r u", u=2))
-    return grouped
+def gather_words(nc, grouped, turned):
+    nc.scalar.copy(out=grouped, in_=turned.rearrange("p (g u) r -> p g r u", u=2))
 
 
-def quantise_words(nc, pool, grouped, n_pass, tag):
-    codes = pool.tile([P, n_pass * P], U32, tag=tag + "_codes", align_bytes=64)
-    scales = pool.tile([P, n_pass * P], U8, tag=tag + "_scales", align_bytes=64)
+def quantise_words(nc, pool, grouped, n, tag):
+    codes = pool.tile([P, n * P], U32, tag=tag + "_codes%d" % n, align_bytes=64)
+    scales = pool.tile([P, n * P], U8, tag=tag + "_scales%d" % n, align_bytes=64)
     nc.vector.quantize_mx(
         out=codes[:].bitcast(FP8X4),
         scales=scales[:],
@@ -79,99 +72,31 @@ def tile_bloomattention_pa_kernel(tc, q, k, v, w_out, b_out, out):
     with ExitStack() as ctx:
         const = ctx.enter_context(tc.tile_pool(name="const", bufs=1))
         loads = ctx.enter_context(tc.tile_pool(name="loads", bufs=3))
-        heads = ctx.enter_context(tc.tile_pool(name="heads", bufs=2))
+        heads = ctx.enter_context(tc.tile_pool(name="heads", bufs=3))
         blocks = ctx.enter_context(tc.tile_pool(name="blocks", bufs=3))
-        near_psum = ctx.enter_context(tc.psum_pool(name="near_psum", bufs=1))
-        far_psum = ctx.enter_context(tc.psum_pool(name="far_psum", bufs=2))
+        score_psum = ctx.enter_context(tc.psum_pool(name="score_psum", bufs=5))
         turn_psum = ctx.enter_context(tc.psum_pool(name="turn_psum", bufs=3))
-        context_psum = ctx.enter_context(tc.psum_pool(name="context_psum", bufs=2))
 
         ident_bf = const.tile([P, P], BF16, name="ident_bf")
         make_identity(nc, ident_bf[:])
         ident_f32 = const.tile([P, P], F32, name="ident_f32")
         make_identity(nc, ident_f32[:])
 
-        distance_int = const.tile([P, BANK], I32, name="distance_int")
-        nc.gpsimd.iota(distance_int[:], pattern=[[-1, BANK]], base=BANK - P, channel_multiplier=1)
-        distance = const.tile([P, BANK], F32, name="distance")
+        distance_int = const.tile([P, S], I32, name="distance_int")
+        nc.gpsimd.iota(distance_int[:], pattern=[[1, S]], base=0, channel_multiplier=-1)
+        distance = const.tile([P, S], F32, name="distance")
         nc.vector.tensor_copy(out=distance[:], in_=distance_int[:])
         nc.gpsimd.affine_select(
-            out=distance[:, BANK - P :],
-            in_=distance[:, BANK - P :],
-            pattern=[[-1, P]],
+            out=distance[:, :P],
+            in_=distance[:, :P],
+            pattern=[[1, P]],
             compare_op=ALU.is_ge,
             fill=MASKED,
             base=0,
-            channel_multiplier=1,
+            channel_multiplier=-1,
         )
-        penalty = []
-        for h in range(NH):
-            strip = const.tile([P, BANK], F32, name="penalty%d" % h)
-            nc.vector.tensor_scalar(
-                out=strip[:], in0=distance[:], scalar1=2.0 ** -(h + 1), scalar2=None, op0=ALU.mult
-            )
-            penalty.append(strip)
 
-        root_left = const.tile([P, PIECES], F32, name="root_left")
-        root = const.tile([P, PIECES], BF16, name="root")
-        nc.vector.tensor_scalar(
-            out=root_left[:, 0:1], in0=ident_f32[:, 0:1], scalar1=0.0, scalar2=HD ** 0.5, op0=ALU.mult, op1=ALU.add
-        )
-        for r in range(PIECES):
-            nc.vector.tensor_copy(out=root[:, r : r + 1], in_=root_left[:, r : r + 1])
-            if r + 1 < PIECES:
-                nc.vector.tensor_tensor(
-                    out=root_left[:, r + 1 : r + 2],
-                    in0=root_left[:, r : r + 1],
-                    in1=root[:, r : r + 1],
-                    op=ALU.subtract,
-                )
-        block_start = const.tile([P, HALF], I32, name="block_start")
-        nc.gpsimd.iota(block_start[:], pattern=[[P, HALF]], base=0, channel_multiplier=0)
-        lane = const.tile([P, HALF], I32, name="lane")
-        nc.gpsimd.iota(lane[:], pattern=[[0, HALF]], base=0, channel_multiplier=1)
-        by_query = const.tile([P, HALF, P], BF16, name="by_query")
-        by_key = const.tile([P, HALF, P], BF16, name="by_key")
-        nc.vector.memset(by_query[:], 0.0)
-        nc.vector.memset(by_key[:], 0.0)
-        query_rows = by_query[:].rearrange("p b (r s) -> p b r s", s=4)
-        key_rows = by_key[:].rearrange("p b (r s) -> p b r s", s=4)
-        pieces = root[:].unsqueeze(1).unsqueeze(3).to_broadcast([P, HALF, PIECES, 2])
-        nc.vector.tensor_copy(out=query_rows[:, :, 0:PIECES, 0:2], in_=pieces)
-        nc.vector.tensor_copy(out=key_rows[:, :, 0:PIECES, 2:4], in_=pieces)
-        starts = block_start[:].unsqueeze(2).to_broadcast([P, HALF, PIECES])
-        lanes = lane[:].unsqueeze(2).to_broadcast([P, HALF, PIECES])
-        nc.vector.tensor_scalar(
-            out=key_rows[:, :, 0:PIECES, 0], in0=starts, scalar1=1.0, scalar2=float(P - BANK), op0=ALU.mult, op1=ALU.add
-        )
-        nc.vector.tensor_scalar(
-            out=key_rows[:, :, 0:PIECES, 1], in0=lanes, scalar1=1.0, scalar2=float(1 - P), op0=ALU.mult, op1=ALU.add
-        )
-        nc.vector.tensor_scalar(
-            out=query_rows[:, :, 0:PIECES, 2], in0=starts, scalar1=-1.0, scalar2=0.0, op0=ALU.mult, op1=ALU.add
-        )
-        nc.vector.tensor_scalar(
-            out=query_rows[:, :, 0:PIECES, 3], in0=lanes, scalar1=-1.0, scalar2=-1.0, op0=ALU.mult, op1=ALU.add
-        )
-        far_keys = const.tile([P, BANK], BF16, name="far_keys")
-        far_unit = const.tile([P, BANK], BF16, name="far_unit")
-        far_queries = []
-        for h in range(NH):
-            sloped = const.tile([P, BANK], BF16, name="far_queries%d" % h)
-            far_queries.append(sloped)
-
-        def turn_far_operands():
-            for by_position, by_row in ((by_key, far_keys), (by_query, far_unit)):
-                turned = turn_psum.tile([P, BANK], BF16, tag="turn")
-                for blk in range(HALF):
-                    nc.tensor.transpose(turned[:, blk * P : (blk + 1) * P], by_position[:, blk, :], ident_bf[:])
-                nc.vector.tensor_copy(out=by_row[:], in_=turned[:])
-            for h in range(NH):
-                nc.vector.tensor_scalar(
-                    out=far_queries[h][:], in0=far_unit[:], scalar1=2.0 ** -(h + 1), scalar2=None, op0=ALU.mult
-                )
-
-        e_sets = []
+        e_sets, far_sums = [], []
         for copy in range(2):
             e_tiles = []
             for n in range(Q_BLOCKS):
@@ -180,6 +105,9 @@ def tile_bloomattention_pa_kernel(tc, q, k, v, w_out, b_out, out):
                     nc.vector.memset(e_tile[:, P * (n + 1) :], 0.0)
                 e_tiles.append(e_tile)
             e_sets.append(e_tiles)
+            far_sum = const.tile([P, Q_BLOCKS], F32, name="far_sum%d" % copy)
+            nc.vector.memset(far_sum[:], 0.0)
+            far_sums.append(far_sum)
 
         w_rows = const.tile([P, H // P, DO], BF16, name="w_rows")
         w_grouped = const.tile([P, H // K_PASS, DO, 4], BF16, name="w_grouped", align_bytes=64)
@@ -187,12 +115,12 @@ def tile_bloomattention_pa_kernel(tc, q, k, v, w_out, b_out, out):
         w_scales = const.tile([P, H // K_PASS, DO], U8, name="w_scales", align_bytes=64)
         bias = const.tile([P, DO], BF16, name="bias")
 
-        q_rows, k_rows, v_rows, q_cols, k_cols = {}, {}, {}, {}, {}
+        q_rows, k_rows, v_rows, turned_rows, q_cols, k_cols = {}, {}, {}, {}, {}, {}
         v_grouped, v_codes, v_scales = {}, {}, {}
-        cost_min, near_min, far_max, near_sum, far_sum, row_scale = {}, {}, {}, {}, {}, {}
+        stats, row_scale, penalty = {}, {}, {}
         c_rows, context = {}, {}
-        near_bank, far_bank, cost, e_turned, e_grouped, e_codes, e_scales = {}, {}, {}, {}, {}, {}, {}
-        c_turned, c_grouped, c_codes, c_scales = {}, {}, {}, {}
+        banks, e_turned, e_grouped, e_codes, e_scales = {}, {}, {}, {}, {}
+        c_turned, c_grouped, c_codes, c_scales, products, results = {}, {}, {}, {}, {}, {}
 
         def load_head(head):
             b, h = divmod(head, NH)
@@ -207,23 +135,45 @@ def tile_bloomattention_pa_kernel(tc, q, k, v, w_out, b_out, out):
             )
             q_rows[head], k_rows[head], v_rows[head] = q_tile, k_tile, v_tile
 
+        def make_penalty(head):
+            strip = heads.tile([P, S], F32, tag="penalty")
+            nc.gpsimd.tensor_scalar(
+                out=strip[:],
+                in0=distance[:],
+                scalar1=-(HD ** 0.5) * 2.0 ** -(head % NH + 1),
+                scalar2=0.0,
+                op0=ALU.mult,
+                op1=ALU.add,
+            )
+            penalty[head] = strip
+
         def turn_rows(rows, tag):
             turned = turn_psum.tile([P, S], BF16, tag="turn")
             for n in range(Q_BLOCKS):
                 nc.tensor.transpose(turned[:, n * P : (n + 1) * P], rows[:, n, :], ident_bf[:])
+            turned_rows[tag] = turned
+
+        def copy_columns(tag):
             columns = heads.tile([P, S], BF16, tag=tag)
-            nc.scalar.copy(out=columns[:], in_=turned[:])
+            nc.scalar.copy(out=columns[:], in_=turned_rows[tag][:])
             return columns
 
         def turn_q(head):
-            q_cols[head] = turn_rows(q_rows[head], "q_cols")
+            turn_rows(q_rows[head], "q_cols")
+
+        def copy_q(head):
+            q_cols[head] = copy_columns("q_cols")
 
         def turn_k(head):
-            k_cols[head] = turn_rows(k_rows[head], "k_cols")
+            turn_rows(k_rows[head], "k_cols")
+
+        def copy_k(head):
+            k_cols[head] = copy_columns("k_cols")
 
         def regroup_v(head):
             grouped = heads.tile([P, S // K_PASS, HD, 4], BF16, tag="v_grouped", align_bytes=64)
-            regroup(nc, v_rows[head][:], grouped[:])
+            for g in range(S // K_PASS):
+                regroup(nc, v_rows[head][:, 4 * g : 4 * g + 4, :], grouped[:, g : g + 1, :, :])
             v_grouped[head] = grouped
 
         def quantise_v(head):
@@ -236,229 +186,323 @@ def tile_bloomattention_pa_kernel(tc, q, k, v, w_out, b_out, out):
             )
             v_codes[head], v_scales[head] = codes, scales
 
-        def near_scores(item):
-            head, n = divmod(item, Q_BLOCKS)
-            near_0, near_n = n // HALF * BANK, (n % HALF + 1) * P
-            near = near_psum.tile([P, BANK], F32, tag="near")
-            nc.tensor.matmul(
-                out=near[:, :near_n],
-                lhsT=q_cols[head][:, n * P : (n + 1) * P],
-                rhs=k_cols[head][:, near_0 : near_0 + near_n],
-                start=True,
-                stop=True,
-            )
-            near_bank[item] = near
+        place = [(head, a) for head in range(HEADS - TURNS) for a in range(UNITS)]
+        for first in range(0, UNITS, 2):
+            place += [(head, a) for head in range(HEADS - TURNS, HEADS) for a in range(first, first + 2)]
+        first_unit = [place.index((head, 0)) for head in range(HEADS)]
 
-        def far_scores(item):
-            head, n = divmod(item, Q_BLOCKS)
-            if n < HALF:
-                return
-            far = far_psum.tile([P, BANK], F32, tag="far")
+        def column(n):
+            return (0, 1, HALF, HALF + 1, HALF + 2, HALF + 3, 2, 3)[n]
+
+        def scores(bank, head, n, first, count):
+            for blk in range(count):
+                back = n - first - blk
+                nc.tensor.matmul(
+                    out=bank[:, blk * P : (blk + 1) * P],
+                    lhsT=penalty[head][:, back * P : (back + 1) * P],
+                    rhs=ident_f32[:],
+                    start=(blk == 0),
+                    stop=False,
+                    is_transpose=True,
+                )
             nc.tensor.matmul(
-                out=far[:], lhsT=q_cols[head][:, n * P : (n + 1) * P], rhs=k_cols[head][:, :BANK], start=True, stop=False
-            )
-            nc.tensor.matmul(
-                out=far[:],
-                lhsT=far_queries[head % NH][:, (n - HALF) * P : (n - HALF + 1) * P],
-                rhs=far_keys[:],
+                out=bank[:, : count * P],
+                lhsT=q_cols[head][:, n * P : (n + 1) * P],
+                rhs=k_cols[head][:, first * P : (first + count) * P],
                 start=False,
                 stop=True,
             )
-            far_bank[item] = far
 
-        def costs(item):
-            head, n = divmod(item, Q_BLOCKS)
-            near_n = (n % HALF + 1) * P
-            if n == 0:
-                lowest = heads.tile([P, Q_BLOCKS], F32, tag="cost_min")
-                lowest_near = heads.tile([P, HALF], F32, tag="near_min")
-                highest_far = heads.tile([P, HALF], F32, tag="far_max")
-                sums_near = heads.tile([P, Q_BLOCKS], F32, tag="near_sum")
-                sums_far = heads.tile([P, HALF], F32, tag="far_sum")
+        def near_scores(unit, far):
+            head, a = place[unit]
+            n = Q_BLOCKS - 1 - a if far else a
+            if far and a == 0:
+                tile = heads.tile([P, 4, Q_BLOCKS], F32, tag="stats")
                 factors = heads.tile([P, Q_BLOCKS], F32, tag="row_scale")
-                cost_min[head], near_min[head], far_max[head] = lowest, lowest_near, highest_far
-                near_sum[head], far_sum[head], row_scale[head] = sums_near, sums_far, factors
-            t = blocks.tile([P, BANK], F32, tag="cost", bufs=4)
-            nc.vector.scalar_tensor_tensor(
-                out=t[:, :near_n],
-                in0=near_bank[item][:, :near_n],
-                scalar=-SCALE,
-                in1=penalty[head % NH][:, BANK - near_n :],
-                op0=ALU.mult,
-                op1=ALU.add,
+                stats[head], row_scale[head] = tile, factors
+            near = score_psum.tile([P, BANK], F32, tag="score")
+            scores(near, head, n, n // HALF * HALF, n % HALF + 1)
+            banks[unit, far] = near
+
+        def near_scores_a(unit):
+            near_scores(unit, 0)
+
+        def near_scores_b(unit):
+            near_scores(unit, 1)
+
+        def far_scores(unit):
+            head, a = place[unit]
+            n = Q_BLOCKS - 1 - a
+            far = score_psum.tile([P, BANK], F32, tag="score")
+            scores(far, head, n, 0, HALF)
+            banks[unit, 2] = far
+
+        def maximum_a(unit):
+            head, a = place[unit]
+            nc.vector.tensor_reduce(
+                out=stats[head][:, 0, column(a) : column(a) + 1], in_=banks[unit, 0][:, : (a + 1) * P], axis=ROW, op=ALU.max
             )
-            cost[item] = t
 
-        def minima(item):
-            head, n = divmod(item, Q_BLOCKS)
-            near_n = (n % HALF + 1) * P
-            if n < HALF:
-                nc.vector.tensor_reduce(out=cost_min[head][:, n : n + 1], in_=cost[item][:, :near_n], axis=ROW, op=ALU.min)
-            else:
-                m = n - HALF
-                nc.vector.tensor_reduce(out=near_min[head][:, m : m + 1], in_=cost[item][:, :near_n], axis=ROW, op=ALU.min)
-                nc.vector.tensor_reduce(out=far_max[head][:, m : m + 1], in_=far_bank[item][:], axis=ROW, op=ALU.max)
+        def shift_a(unit):
+            head, a = place[unit]
+            nc.vector.tensor_scalar(
+                out=stats[head][:, 2, column(a) : column(a) + 1], in0=stats[head][:, 0, column(a) : column(a) + 1], scalar1=-SCALE, scalar2=None, op0=ALU.mult
+            )
 
-        def join_minima(item):
-            head, n = divmod(item, Q_BLOCKS)
-            if n >= HALF:
-                m = n - HALF
-                nc.vector.tensor_scalar(
-                    out=cost_min[head][:, n : n + 1],
-                    in0=far_max[head][:, m : m + 1],
-                    scalar1=-SCALE,
-                    scalar2=near_min[head][:, m : m + 1],
-                    op0=ALU.mult,
-                    op1=ALU.min,
-                )
+        def maximum_b(unit):
+            head, a = place[unit]
+            n = Q_BLOCKS - 1 - a
+            nc.vector.tensor_reduce(
+                out=stats[head][:, 0, column(n) : column(n) + 1], in_=banks[unit, 1][:, : (HALF - a) * P], axis=ROW, op=ALU.max
+            )
 
-        def exponentials(item):
-            head, n = divmod(item, Q_BLOCKS)
-            near_0, near_n = n // HALF * BANK, (n % HALF + 1) * P
-            e_tile = e_sets[head % 2][n]
-            if n >= HALF:
-                nc.scalar.activation(
-                    out=e_tile[:, :BANK],
-                    in_=far_bank[item][:],
-                    func=ACT.Exp,
-                    bias=cost_min[head][:, n : n + 1],
-                    scale=SCALE,
-                    accum_out=far_sum[head][:, n - HALF : n - HALF + 1],
-                )
+        def maximum_far(unit):
+            head, a = place[unit]
+            n = Q_BLOCKS - 1 - a
+            nc.vector.tensor_reduce(out=stats[head][:, 1, column(n) : column(n) + 1], in_=banks[unit, 2][:], axis=ROW, op=ALU.max)
+
+        def shift_b(unit):
+            head, a = place[unit]
+            n = Q_BLOCKS - 1 - a
+            nc.vector.tensor_scalar(
+                out=stats[head][:, 2, column(n) : column(n) + 1],
+                in0=stats[head][:, 0, column(n) : column(n) + 1],
+                scalar1=stats[head][:, 1, column(n) : column(n) + 1],
+                scalar2=-SCALE,
+                op0=ALU.max,
+                op1=ALU.mult,
+            )
+
+        def exponential(unit, n, bank, first, width, sums):
+            head = place[unit][0]
             nc.scalar.activation(
-                out=e_tile[:, near_0 : near_0 + near_n],
-                in_=cost[item][:, :near_n],
+                out=e_sets[head % 2][n][:, first : first + width],
+                in_=bank[:, :width],
                 func=ACT.Exp,
-                bias=cost_min[head][:, n : n + 1],
-                scale=-1.0,
-                accum_out=near_sum[head][:, n : n + 1],
+                bias=stats[head][:, 2, column(n) : column(n) + 1],
+                scale=SCALE,
+                accum_out=sums[:, column(n) : column(n) + 1],
             )
 
-        def turn_e(item):
-            head, n = divmod(item, Q_BLOCKS)
-            e_turned[item] = turn_words(nc, turn_psum, e_sets[head % 2][n][:], n // HALF + 1, ident_f32[:])
+        def exponential_a(unit):
+            head, a = place[unit]
+            exponential(unit, a, banks[unit, 0], 0, (a + 1) * P, stats[head][:, 3, :])
 
-        def gather_e(item):
-            e_grouped[item] = gather_words(nc, blocks, e_turned[item], item % Q_BLOCKS // HALF + 1, "e")
+        def exponential_b(unit):
+            head, a = place[unit]
+            exponential(unit, Q_BLOCKS - 1 - a, banks[unit, 1], BANK, (HALF - a) * P, stats[head][:, 3, :])
 
-        def quantise_e(item):
-            head, n = divmod(item, Q_BLOCKS)
-            if n == Q_BLOCKS - 1:
-                nc.vector.tensor_tensor(
-                    out=row_scale[head][:, HALF:], in0=near_sum[head][:, HALF:], in1=far_sum[head][:], op=ALU.add
-                )
-            e_codes[item], e_scales[item] = quantise_words(nc, blocks, e_grouped[item], n // HALF + 1, "e")
-            if n == HALF - 1:
-                nc.vector.reciprocal(out=row_scale[head][:, :HALF], in_=near_sum[head][:, :HALF])
-            if n == Q_BLOCKS - 1:
-                nc.vector.reciprocal(out=row_scale[head][:, HALF:], in_=row_scale[head][:, HALF:])
+        def exponential_far(unit):
+            head, a = place[unit]
+            n = Q_BLOCKS - 1 - a
+            exponential(unit, n, banks[unit, 2], 0, BANK, far_sums[head % 2])
 
-        def contexts(item):
-            head, n = divmod(item, Q_BLOCKS)
-            if n % HALF == 0:
-                bank = context_psum.tile([P, HALF, HD], F32, tag="context")
-                context[item // HALF] = bank
-            for g in range(n // HALF + 1):
-                nc.tensor.matmul_mx(
-                    out=context[item // HALF][:, n % HALF, :],
-                    lhsT=e_codes[item][:, g * P : (g + 1) * P].bitcast(FP8X4),
-                    lhsT_scale=e_scales[item][:, g * P : (g + 1) * P],
-                    rhs=v_codes[head][:, g, :].bitcast(FP8X4),
-                    rhs_scale=v_scales[head][:, g, :],
-                    start=(g == 0),
-                    stop=(g == n // HALF),
-                )
+        def turn_a(unit):
+            head, a = place[unit]
+            if a % 2 == 1:
+                turned = turn_psum.tile([P, HALF, P], F32, tag="turn")
+                e_turned[unit // 2, 0] = turned
+                for m in range(2):
+                    turn_words(nc, turned[:, 2 * m : 2 * m + 2, :], e_sets[head % 2][a - 1 + m][:], 1, ident_f32[:])
 
-        def normalise(item):
-            head, n = divmod(item, Q_BLOCKS)
+        def turn_b(unit):
+            head, a = place[unit]
+            turned = turn_psum.tile([P, HALF, P], F32, tag="turn")
+            e_turned[unit, 1] = turned
+            turn_words(nc, turned[:], e_sets[head % 2][Q_BLOCKS - 1 - a][:], 2, ident_f32[:])
+
+        def gather_a(unit):
+            if unit % 2 == 1:
+                pair = blocks.tile([P, 2, P, 2], F32, tag="e_grouped_a", align_bytes=64)
+                e_grouped[unit // 2, 0] = pair
+                gather_words(nc, pair[:], e_turned[unit // 2, 0][:])
+
+        def gather_b(unit):
+            if unit % 2 == 0:
+                pair = blocks.tile([P, 4, P, 2], F32, tag="e_grouped_b", align_bytes=64)
+                e_grouped[unit // 2, 1] = pair
+            first = 2 - 2 * (unit % 2)
+            gather_words(nc, e_grouped[unit // 2, 1][:, first : first + 2, :, :], e_turned[unit, 1][:])
+
+        def quantise_a(unit):
+            if unit % 2 == 1:
+                e_codes[unit // 2, 0], e_scales[unit // 2, 0] = quantise_words(nc, blocks, e_grouped[unit // 2, 0], 2, "e_a")
+
+        def quantise_b(unit):
+            if unit % 2 == 1:
+                e_codes[unit // 2, 1], e_scales[unit // 2, 1] = quantise_words(nc, blocks, e_grouped[unit // 2, 1], 4, "e_b")
+
+        def half_rows(tile, half):
+            pairs = tile.rearrange("p (x y) d -> p x y d", y=2)
+            return pairs[:, 1:3] if half else pairs[:, 0::3]
+
+        def contexts(unit):
+            head, a = place[unit]
+            if a % 2 == 0:
+                return
+            half = unit // 2
+            bank = turn_psum.tile([P, HALF, HD], F32, tag="turn")
+            context[half] = bank
+            for m in range(HALF):
+                part, n_pass = m // 2, m // 2 + 1
+                for g in range(n_pass):
+                    first = (m % 2 * n_pass + g) * P
+                    nc.tensor.matmul_mx(
+                        out=bank[:, m, :],
+                        lhsT=e_codes[half, part][:, first : first + P].bitcast(FP8X4),
+                        lhsT_scale=e_scales[half, part][:, first : first + P],
+                        rhs=v_codes[head][:, g, :].bitcast(FP8X4),
+                        rhs_scale=v_scales[head][:, g, :],
+                        start=(g == 0),
+                        stop=(g == n_pass - 1),
+                    )
+
+        def row_sums(unit):
+            head, a = place[unit]
+            if a % 2 == 0:
+                return
+            four = slice(a // 2 * HALF, a // 2 * HALF + HALF)
+            nc.vector.tensor_tensor(
+                out=row_scale[head][:, four], in0=stats[head][:, 3, four], in1=far_sums[head % 2][:, four], op=ALU.add
+            )
+
+        def reciprocals(unit):
+            head, a = place[unit]
+            if a % 2 == 0:
+                return
+            four = slice(a // 2 * HALF, a // 2 * HALF + HALF)
+            nc.vector.reciprocal(out=row_scale[head][:, four], in_=row_scale[head][:, four])
+
+        def normalise(unit):
+            head, a = place[unit]
             b, h = divmod(head, NH)
-            if n % HALF != HALF - 1:
+            if a % 2 == 0:
                 return
-            if h == 0 and n == HALF - 1:
-                rows = heads.tile([P, Q_BLOCKS, H], BF16, tag="c_rows")
+            if h == 0 and a == 1:
+                rows = heads.tile([P, Q_BLOCKS, H], BF16, tag="c_rows", bufs=2)
                 c_rows[b] = rows
-            for m in range(n - (HALF - 1), n + 1):
-                nc.scalar.activation(
-                    out=c_rows[b][:, m, h * HD : (h + 1) * HD],
-                    in_=context[item // HALF][:, m % HALF, :],
-                    func=ACT.Copy,
-                    scale=row_scale[head][:, m : m + 1],
-                )
+            factors = row_scale[head][:, a // 2 * HALF : a // 2 * HALF + HALF]
+            nc.vector.tensor_tensor(
+                out=half_rows(c_rows[b][:, :, h * HD : (h + 1) * HD], a // 2),
+                in0=context[unit // 2][:].rearrange("p (x y) d -> p x y d", y=2),
+                in1=factors.rearrange("p (x y) -> p x y", y=2).unsqueeze(3).to_broadcast([P, 2, 2, HD]),
+                op=ALU.mult,
+            )
 
-        def turn_c(item):
-            head, n = divmod(item, Q_BLOCKS)
-            if head % NH == NH - 1:
-                c_turned[item] = turn_words(nc, turn_psum, c_rows[head // NH][:, n, :], H // K_PASS, ident_f32[:])
-                c_grouped[item] = gather_words(nc, blocks, c_turned[item], H // K_PASS, "c")
+        def turn_c(block):
+            b, n = block
+            turned = turn_psum.tile([P, HALF, P], F32, tag="turn")
+            turn_words(nc, turned[:], c_rows[b][:, n, :], H // K_PASS, ident_f32[:])
+            c_turned[block] = turned
 
-        def quantise_c(item):
-            if item // Q_BLOCKS % NH == NH - 1:
-                c_codes[item], c_scales[item] = quantise_words(nc, blocks, c_grouped[item], H // K_PASS, "c")
+        def gather_c(block):
+            grouped = blocks.tile([P, H // K_PASS, P, 2], F32, tag="c_grouped", align_bytes=64)
+            gather_words(nc, grouped[:], c_turned[block][:])
+            c_grouped[block] = grouped
 
-        def project(item):
-            head, n = divmod(item, Q_BLOCKS)
-            if head % NH != NH - 1:
-                return
-            result = blocks.tile([P, DO], F32, tag="result")
-            for n0 in range(0, DO, BANK):
-                product = turn_psum.tile([P, BANK], F32, tag="turn")
+        def quantise_c(block):
+            c_codes[block], c_scales[block] = quantise_words(nc, blocks, c_grouped[block], H // K_PASS, "c")
+
+        def project(block, n0):
+            b, n = block
+            if n0 == 0:
+                result = blocks.tile([P, DO], F32, tag="result", bufs=5)
+                results[block] = result
+            if True:
+                if b == B - 1:
+                    product = score_psum.tile([P, BANK], F32, tag="score")
+                else:
+                    product = turn_psum.tile([P, BANK], F32, tag="turn")
                 for g in range(H // K_PASS):
                     nc.tensor.matmul_mx(
                         out=product[:],
-                        lhsT=c_codes[item][:, g * P : (g + 1) * P].bitcast(FP8X4),
-                        lhsT_scale=c_scales[item][:, g * P : (g + 1) * P],
+                        lhsT=c_codes[block][:, g * P : (g + 1) * P].bitcast(FP8X4),
+                        lhsT_scale=c_scales[block][:, g * P : (g + 1) * P],
                         rhs=w_codes[:, g, n0 : n0 + BANK].bitcast(FP8X4),
                         rhs_scale=w_scales[:, g, n0 : n0 + BANK],
                         start=(g == 0),
                         stop=(g == H // K_PASS - 1),
                     )
-                nc.vector.tensor_tensor(
-                    out=result[:, n0 : n0 + BANK], in0=product[:], in1=bias[:, n0 : n0 + BANK], op=ALU.add
-                )
-            nc.sync.dma_start(out=out[head // NH, n * P : (n + 1) * P, :], in_=result[:])
+            products[block, n0] = product
 
-        def for_item(stage, item):
-            if 0 <= item < ITEMS:
-                stage(item)
+        def add_bias(block, n0):
+            b, n = block
+            nc.vector.tensor_tensor(
+                out=results[block][:, n0 : n0 + BANK], in0=products[block, n0][:], in1=bias[:, n0 : n0 + BANK], op=ALU.add
+            )
+            if n0 + BANK == DO:
+                nc.sync.dma_start(out=out[b, n * P : (n + 1) * P, :], in_=results[block][:])
+
+        project_at = {}
+        for b in range(B):
+            for half in range(2):
+                for m, n in enumerate(((0, 1, 6, 7), (2, 3, 4, 5))[half]):
+                    ready = place.index((b * NH + NH - 1, 2 * half + 1)) + PROJECT_LAG
+                    project_at[b, n] = ready + PROJECT_EVERY * (HALF * half + m) if b + 1 < B else ready + m
+
+        def for_unit(stage, unit):
+            if 0 <= unit < len(place):
+                stage(unit)
 
         def for_head(prepare, step):
-            if step % Q_BLOCKS == 0 and 0 <= step // Q_BLOCKS < HEADS:
-                prepare(step // Q_BLOCKS)
+            if step in first_unit:
+                prepare(first_unit.index(step))
 
-        for step in range(-LOAD_LEAD, ITEMS + PROJECT_LAG + 3):
-            for_item(turn_e, step - 4)
-            for_item(contexts, step - 6)
-            for_item(near_scores, step)
-            for_item(far_scores, step - 1)
-            for_item(costs, step - 1)
-            for_item(minima, step - 2)
-            for_item(quantise_e, step - 5)
-            for_item(join_minima, step - 2)
-            for_item(exponentials, step - 3)
-            for_item(gather_e, step - 4)
-            for_item(normalise, step - 7)
-            for_item(turn_c, step - PROJECT_LAG)
-            for_item(quantise_c, step - PROJECT_LAG - 1)
-            for_item(project, step - PROJECT_LAG - 2)
-            for_head(load_head, step + LOAD_LEAD)
-            for_head(regroup_v, step + V_REGROUP_LEAD)
-            for_head(turn_q, step + Q_TURN_LEAD)
-            for_head(turn_k, step + K_TURN_LEAD)
-            for_head(quantise_v, step + V_QUANTISE_LEAD)
-            if step == -1:
-                turn_far_operands()
-            if step == 0:
-                nc.sync.dma_start(
-                    out=w_rows[:].rearrange("p (c e) n -> p c (e n)", e=2),
-                    in_=w_out.rearrange("(c p e) n -> p c (e n)", p=P, e=2),
-                )
-                nc.sync.dma_start(out=bias[:], in_=b_out.partition_broadcast(P))
-            for g in range(H // K_PASS):
-                if step == W_STEP + 2 * g * Q_BLOCKS:
-                    regroup(nc, w_rows[:, 4 * g : 4 * g + 4, :], w_grouped[:, g : g + 1, :, :])
-                if step == W_STEP + (2 * g + 1) * Q_BLOCKS:
-                    nc.vector.quantize_mx(
-                        out=w_codes[:, g, :].bitcast(FP8X4),
-                        scales=w_scales[:, g, :],
-                        in_=w_grouped[:, g, :, :].rearrange("p n t -> p (n t)"),
+        def for_tokens(stage, step, *columns):
+            for block in project_at:
+                if project_at[block] == step:
+                    stage(block, *columns)
+
+        with tc.manual_schedule():
+            for step in range(-LOAD_LEAD, HEADS * UNITS + PROJECT_LAG + 8):
+                for_unit(row_sums, step - 1)
+                for_unit(quantise_b, step - 1)
+                for_unit(reciprocals, step - 1)
+                for_unit(maximum_b, step + 1)
+                for_unit(exponential_b, step)
+                for_unit(maximum_far, step + 1)
+                for_unit(near_scores_a, step + 1)
+                for_unit(exponential_far, step)
+                for_unit(turn_b, step)
+                for_unit(gather_a, step - 1)
+                for_head(copy_q, step + 3)
+                for_head(copy_k, step + 5)
+                for_tokens(gather_c, step - 1)
+                for_unit(exponential_a, step)
+                for_tokens(add_bias, step - 3, 0)
+                for_unit(maximum_a, step + 1)
+                for_unit(shift_b, step + 1)
+                for_head(quantise_v, step)
+                for_unit(quantise_a, step - 1)
+                for_unit(shift_a, step + 1)
+                for_tokens(quantise_c, step - 1)
+                for_unit(near_scores_b, step + 2)
+                for_unit(contexts, step - 2)
+                for_tokens(project, step - 2, 0)
+                for_tokens(project, step - 2, BANK)
+                for_unit(far_scores, step + 2)
+                for_unit(turn_a, step)
+                for_unit(gather_b, step)
+                for_head(turn_q, step + 4)
+                for_head(turn_k, step + 6)
+                for_unit(normalise, step - 2)
+                for_tokens(turn_c, step)
+                for_tokens(add_bias, step - 3, BANK)
+                for_head(load_head, step + 10)
+                for_head(make_penalty, step + 6)
+                for_head(regroup_v, step + 3)
+                if step == 0:
+                    nc.sync.dma_start(
+                        out=w_rows[:].rearrange("p (c e) n -> p c (e n)", e=2),
+                        in_=w_out.rearrange("(c p e) n -> p c (e n)", p=P, e=2),
                     )
+                    nc.sync.dma_start(out=bias[:], in_=b_out.partition_broadcast(P))
+                for g in range(H // K_PASS):
+                    if step == W_STEP + 2 * g * UNITS:
+                        regroup(nc, w_rows[:, 4 * g : 4 * g + 4, :], w_grouped[:, g : g + 1, :, :])
+                    if step == W_STEP + (2 * g + 1) * UNITS:
+                        nc.vector.quantize_mx(
+                            out=w_codes[:, g, :].bitcast(FP8X4),
+                            scales=w_scales[:, g, :],
+                            in_=w_grouped[:, g, :, :].rearrange("p n t -> p (n t)"),
+                        )

@@ -21,7 +21,7 @@ K_PASS = 512
 Q_BLOCKS = S // P
 HALF = K_PASS // P
 SCALE = HD ** -0.5
-MASKED = 1.0e30
+MASKED = -1.0e30
 
 FLOPS = 2 * 2 * B * NH * HD * (K_PASS * K_PASS + K_PASS * S) + 2 * B * S * H * DO
 
@@ -29,10 +29,12 @@ HEADS = B * NH
 UNITS = Q_BLOCKS // 2
 
 LOAD_LEAD = 10
-W_STEP = 5
+W_STEP = 1
+W_PIECES = 32
+W_QUARTER = W_PIECES // 4
 PROJECT_LAG = 3
 TURNS = 3
-PROJECT_EVERY = 3
+PROJECT_EVERY = 4
 
 
 def regroup(nc, rows, grouped):
@@ -82,13 +84,15 @@ def tile_bloomattention_pa_kernel(tc, q, k, v, w_out, b_out, out):
         ident_f32 = const.tile([P, P], F32, name="ident_f32")
         make_identity(nc, ident_f32[:])
 
-        distance_int = const.tile([P, S], I32, name="distance_int")
-        nc.gpsimd.iota(distance_int[:], pattern=[[1, S]], base=0, channel_multiplier=-1)
-        distance = const.tile([P, S], F32, name="distance")
-        nc.vector.tensor_copy(out=distance[:], in_=distance_int[:])
+        distance = const.tile([P, S], I32, name="distance")
+        nc.gpsimd.iota(distance[:], pattern=[[1, S]], base=0, channel_multiplier=-1)
+        penalty = const.tile([P, S], F32, name="penalty")
+        nc.vector.tensor_scalar(
+            out=penalty[:], in0=distance[:], scalar1=-(HD ** 0.5), scalar2=None, op0=ALU.mult
+        )
         nc.gpsimd.affine_select(
-            out=distance[:, :P],
-            in_=distance[:, :P],
+            out=penalty[:, :P],
+            in_=penalty[:, :P],
             pattern=[[1, P]],
             compare_op=ALU.is_ge,
             fill=MASKED,
@@ -117,7 +121,7 @@ def tile_bloomattention_pa_kernel(tc, q, k, v, w_out, b_out, out):
 
         q_rows, k_rows, v_rows, turned_rows, q_cols, k_cols = {}, {}, {}, {}, {}, {}
         v_grouped, v_codes, v_scales = {}, {}, {}
-        stats, row_scale, penalty = {}, {}, {}
+        stats, row_scale = {}, {}
         c_rows, context = {}, {}
         banks, e_turned, e_grouped, e_codes, e_scales = {}, {}, {}, {}, {}
         c_turned, c_grouped, c_codes, c_scales, products, results = {}, {}, {}, {}, {}, {}
@@ -135,45 +139,39 @@ def tile_bloomattention_pa_kernel(tc, q, k, v, w_out, b_out, out):
             )
             q_rows[head], k_rows[head], v_rows[head] = q_tile, k_tile, v_tile
 
-        def make_penalty(head):
-            strip = heads.tile([P, S], F32, tag="penalty")
-            nc.gpsimd.tensor_scalar(
-                out=strip[:],
-                in0=distance[:],
-                scalar1=-(HD ** 0.5) * 2.0 ** -(head % NH + 1),
-                scalar2=0.0,
-                op0=ALU.mult,
-                op1=ALU.add,
-            )
-            penalty[head] = strip
-
         def turn_rows(rows, tag):
             turned = turn_psum.tile([P, S], BF16, tag="turn")
             for n in range(Q_BLOCKS):
                 nc.tensor.transpose(turned[:, n * P : (n + 1) * P], rows[:, n, :], ident_bf[:])
             turned_rows[tag] = turned
 
-        def copy_columns(tag):
-            columns = heads.tile([P, S], BF16, tag=tag)
-            nc.scalar.copy(out=columns[:], in_=turned_rows[tag][:])
-            return columns
+        def slope(head):
+            return 2.0 ** -(head % NH + 1)
 
         def turn_q(head):
             turn_rows(q_rows[head], "q_cols")
 
         def copy_q(head):
-            q_cols[head] = copy_columns("q_cols")
+            columns = heads.tile([P, S], BF16, tag="q_cols")
+            nc.vector.tensor_scalar(
+                out=columns[:], in0=turned_rows["q_cols"][:], scalar1=1.0 / slope(head), scalar2=None, op0=ALU.mult
+            )
+            q_cols[head] = columns
 
         def turn_k(head):
             turn_rows(k_rows[head], "k_cols")
 
         def copy_k(head):
-            k_cols[head] = copy_columns("k_cols")
+            columns = heads.tile([P, S], BF16, tag="k_cols")
+            nc.scalar.copy(out=columns[:], in_=turned_rows["k_cols"][:])
+            k_cols[head] = columns
 
         def regroup_v(head):
             grouped = heads.tile([P, S // K_PASS, HD, 4], BF16, tag="v_grouped", align_bytes=64)
             for g in range(S // K_PASS):
-                regroup(nc, v_rows[head][:, 4 * g : 4 * g + 4, :], grouped[:, g : g + 1, :, :])
+                for d in range(0, HD, HD // 2):
+                    columns = slice(d, d + HD // 2)
+                    regroup(nc, v_rows[head][:, 4 * g : 4 * g + 4, columns], grouped[:, g : g + 1, columns, :])
             v_grouped[head] = grouped
 
         def quantise_v(head):
@@ -185,6 +183,21 @@ def tile_bloomattention_pa_kernel(tc, q, k, v, w_out, b_out, out):
                 in_=v_grouped[head][:].rearrange("p g d t -> p (g d t)"),
             )
             v_codes[head], v_scales[head] = codes, scales
+
+        def regroup_w(piece):
+            g, part = divmod(piece, W_PIECES // 2)
+            width = DO // (W_PIECES // 2)
+            columns = slice(part * width, (part + 1) * width)
+            regroup(nc, w_rows[:, 4 * g : 4 * g + 4, columns], w_grouped[:, g : g + 1, columns, :])
+
+        def quantise_w(quarter):
+            g, part = divmod(quarter, DO // BANK)
+            columns = slice(part * BANK, (part + 1) * BANK)
+            nc.vector.quantize_mx(
+                out=w_codes[:, g, columns].bitcast(FP8X4),
+                scales=w_scales[:, g, columns],
+                in_=w_grouped[:, g, columns, :].rearrange("p n t -> p (n t)"),
+            )
 
         place = [(head, a) for head in range(HEADS - TURNS) for a in range(UNITS)]
         for first in range(0, UNITS, 2):
@@ -199,7 +212,7 @@ def tile_bloomattention_pa_kernel(tc, q, k, v, w_out, b_out, out):
                 back = n - first - blk
                 nc.tensor.matmul(
                     out=bank[:, blk * P : (blk + 1) * P],
-                    lhsT=penalty[head][:, back * P : (back + 1) * P],
+                    lhsT=penalty[:, back * P : (back + 1) * P],
                     rhs=ident_f32[:],
                     start=(blk == 0),
                     stop=False,
@@ -246,7 +259,7 @@ def tile_bloomattention_pa_kernel(tc, q, k, v, w_out, b_out, out):
         def shift_a(unit):
             head, a = place[unit]
             nc.vector.tensor_scalar(
-                out=stats[head][:, 2, column(a) : column(a) + 1], in0=stats[head][:, 0, column(a) : column(a) + 1], scalar1=-SCALE, scalar2=None, op0=ALU.mult
+                out=stats[head][:, 2, column(a) : column(a) + 1], in0=stats[head][:, 0, column(a) : column(a) + 1], scalar1=-SCALE * slope(head), scalar2=None, op0=ALU.mult
             )
 
         def maximum_b(unit):
@@ -268,7 +281,7 @@ def tile_bloomattention_pa_kernel(tc, q, k, v, w_out, b_out, out):
                 out=stats[head][:, 2, column(n) : column(n) + 1],
                 in0=stats[head][:, 0, column(n) : column(n) + 1],
                 scalar1=stats[head][:, 1, column(n) : column(n) + 1],
-                scalar2=-SCALE,
+                scalar2=-SCALE * slope(head),
                 op0=ALU.max,
                 op1=ALU.mult,
             )
@@ -280,7 +293,7 @@ def tile_bloomattention_pa_kernel(tc, q, k, v, w_out, b_out, out):
                 in_=bank[:, :width],
                 func=ACT.Exp,
                 bias=stats[head][:, 2, column(n) : column(n) + 1],
-                scale=SCALE,
+                scale=SCALE * slope(head),
                 accum_out=sums[:, column(n) : column(n) + 1],
             )
 
@@ -455,9 +468,8 @@ def tile_bloomattention_pa_kernel(tc, q, k, v, w_out, b_out, out):
 
         with tc.manual_schedule():
             for step in range(-LOAD_LEAD, HEADS * UNITS + PROJECT_LAG + 8):
-                for_unit(row_sums, step - 1)
-                for_unit(quantise_b, step - 1)
-                for_unit(reciprocals, step - 1)
+                for_tokens(add_bias, step - 3, 0)
+                for_tokens(add_bias, step - 3, BANK)
                 for_unit(maximum_b, step + 1)
                 for_unit(exponential_b, step)
                 for_unit(maximum_far, step + 1)
@@ -465,16 +477,18 @@ def tile_bloomattention_pa_kernel(tc, q, k, v, w_out, b_out, out):
                 for_unit(exponential_far, step)
                 for_unit(turn_b, step)
                 for_unit(gather_a, step - 1)
-                for_head(copy_q, step + 3)
-                for_head(copy_k, step + 5)
+                for_head(copy_k, step + 3)
                 for_tokens(gather_c, step - 1)
                 for_unit(exponential_a, step)
-                for_tokens(add_bias, step - 3, 0)
                 for_unit(maximum_a, step + 1)
+                for_unit(row_sums, step - 1)
                 for_unit(shift_b, step + 1)
-                for_head(quantise_v, step)
-                for_unit(quantise_a, step - 1)
+                for_head(copy_q, step + 5)
+                for_unit(quantise_b, step - 1)
                 for_unit(shift_a, step + 1)
+                for_unit(reciprocals, step - 1)
+                for_unit(quantise_a, step - 1)
+                for_head(quantise_v, step)
                 for_tokens(quantise_c, step - 1)
                 for_unit(near_scores_b, step + 2)
                 for_unit(contexts, step - 2)
@@ -483,26 +497,20 @@ def tile_bloomattention_pa_kernel(tc, q, k, v, w_out, b_out, out):
                 for_unit(far_scores, step + 2)
                 for_unit(turn_a, step)
                 for_unit(gather_b, step)
-                for_head(turn_q, step + 4)
-                for_head(turn_k, step + 6)
+                for_head(turn_q, step + 6)
+                for_head(turn_k, step + 4)
                 for_unit(normalise, step - 2)
                 for_tokens(turn_c, step)
-                for_tokens(add_bias, step - 3, BANK)
                 for_head(load_head, step + 10)
-                for_head(make_penalty, step + 6)
-                for_head(regroup_v, step + 3)
+                for_head(regroup_v, step + 6)
                 if step == 0:
                     nc.sync.dma_start(
                         out=w_rows[:].rearrange("p (c e) n -> p c (e n)", e=2),
                         in_=w_out.rearrange("(c p e) n -> p c (e n)", p=P, e=2),
                     )
                     nc.sync.dma_start(out=bias[:], in_=b_out.partition_broadcast(P))
-                for g in range(H // K_PASS):
-                    if step == W_STEP + 2 * g * UNITS:
-                        regroup(nc, w_rows[:, 4 * g : 4 * g + 4, :], w_grouped[:, g : g + 1, :, :])
-                    if step == W_STEP + (2 * g + 1) * UNITS:
-                        nc.vector.quantize_mx(
-                            out=w_codes[:, g, :].bitcast(FP8X4),
-                            scales=w_scales[:, g, :],
-                            in_=w_grouped[:, g, :, :].rearrange("p n t -> p (n t)"),
-                        )
+                piece = step - W_STEP
+                if 0 <= piece < W_PIECES:
+                    regroup_w(piece)
+                if piece > 0 and piece % W_QUARTER == 0 and piece <= W_PIECES:
+                    quantise_w(piece // W_QUARTER - 1)

@@ -121,7 +121,7 @@ def tile_bloomattention_pa_kernel(tc, q, k, v, w_out, b_out, out):
 
         q_rows, k_rows, v_rows, turned_rows, q_cols, k_cols = {}, {}, {}, {}, {}, {}
         v_grouped, v_codes, v_scales = {}, {}, {}
-        stats, row_scale = {}, {}
+        stats, row_scale, row_sum = {}, {}, {}
         c_rows, context = {}, {}
         banks, e_turned, e_grouped, e_codes, e_scales = {}, {}, {}, {}, {}
         c_turned, c_grouped, c_codes, c_scales, products, results = {}, {}, {}, {}, {}, {}
@@ -232,7 +232,8 @@ def tile_bloomattention_pa_kernel(tc, q, k, v, w_out, b_out, out):
             if far and a == 0:
                 tile = heads.tile([P, 4, Q_BLOCKS], F32, tag="stats")
                 factors = heads.tile([P, Q_BLOCKS], F32, tag="row_scale")
-                stats[head], row_scale[head] = tile, factors
+                sums = heads.tile([P, Q_BLOCKS], F32, tag="row_sum")
+                stats[head], row_scale[head], row_sum[head] = tile, factors, sums
             near = score_psum.tile([P, BANK], F32, tag="score")
             scores(near, head, n, n // HALF * HALF, n % HALF + 1)
             banks[unit, far] = near
@@ -258,8 +259,8 @@ def tile_bloomattention_pa_kernel(tc, q, k, v, w_out, b_out, out):
 
         def shift_a(unit):
             head, a = place[unit]
-            nc.vector.tensor_scalar(
-                out=stats[head][:, 2, column(a) : column(a) + 1], in0=stats[head][:, 0, column(a) : column(a) + 1], scalar1=-SCALE * slope(head), scalar2=None, op0=ALU.mult
+            nc.scalar.activation(
+                out=stats[head][:, 2, column(a) : column(a) + 1], in_=stats[head][:, 0, column(a) : column(a) + 1], func=ACT.Copy, scale=-SCALE * slope(head)
             )
 
         def maximum_b(unit):
@@ -375,8 +376,8 @@ def tile_bloomattention_pa_kernel(tc, q, k, v, w_out, b_out, out):
             if a % 2 == 0:
                 return
             four = slice(a // 2 * HALF, a // 2 * HALF + HALF)
-            nc.vector.tensor_tensor(
-                out=row_scale[head][:, four], in0=stats[head][:, 3, four], in1=far_sums[head % 2][:, four], op=ALU.add
+            nc.gpsimd.tensor_tensor(
+                out=row_sum[head][:, four], in0=stats[head][:, 3, four], in1=far_sums[head % 2][:, four], op=ALU.add
             )
 
         def reciprocals(unit):
@@ -384,7 +385,7 @@ def tile_bloomattention_pa_kernel(tc, q, k, v, w_out, b_out, out):
             if a % 2 == 0:
                 return
             four = slice(a // 2 * HALF, a // 2 * HALF + HALF)
-            nc.vector.reciprocal(out=row_scale[head][:, four], in_=row_scale[head][:, four])
+            nc.vector.reciprocal(out=row_scale[head][:, four], in_=row_sum[head][:, four])
 
         def normalise(unit):
             head, a = place[unit]
@@ -471,6 +472,7 @@ def tile_bloomattention_pa_kernel(tc, q, k, v, w_out, b_out, out):
                 for_tokens(add_bias, step - 3, 0)
                 for_tokens(add_bias, step - 3, BANK)
                 for_unit(maximum_b, step + 1)
+                for_unit(shift_a, step)
                 for_unit(exponential_b, step)
                 for_unit(maximum_far, step + 1)
                 for_unit(near_scores_a, step + 1)
@@ -485,7 +487,6 @@ def tile_bloomattention_pa_kernel(tc, q, k, v, w_out, b_out, out):
                 for_unit(shift_b, step + 1)
                 for_head(copy_q, step + 5)
                 for_unit(quantise_b, step - 1)
-                for_unit(shift_a, step + 1)
                 for_unit(reciprocals, step - 1)
                 for_unit(quantise_a, step - 1)
                 for_head(quantise_v, step)

@@ -478,10 +478,10 @@ def tile_bloomattention_pa_kernel(tc, q, k, v, w_out, b_out, out):
                 for_unit(near_scores_a, step + 1)
                 for_unit(exponential_far, step)
                 for_unit(turn_b, step)
+                for_unit(exponential_a, step)
                 for_unit(gather_a, step - 1)
                 for_head(copy_k, step + 3)
                 for_tokens(gather_c, step - 1)
-                for_unit(exponential_a, step)
                 for_unit(maximum_a, step + 1)
                 for_unit(row_sums, step - 1)
                 for_unit(shift_b, step + 1)
@@ -498,8 +498,8 @@ def tile_bloomattention_pa_kernel(tc, q, k, v, w_out, b_out, out):
                 for_unit(far_scores, step + 2)
                 for_unit(turn_a, step)
                 for_unit(gather_b, step)
-                for_head(turn_q, step + 6)
                 for_head(turn_k, step + 4)
+                for_head(turn_q, step + 6)
                 for_unit(normalise, step - 2)
                 for_tokens(turn_c, step)
                 for_head(load_head, step + 10)

@@ -1,4 +1,5 @@
 from contextlib import ExitStack
+from functools import partial
 
 import concourse.mybir as mybir
 from concourse.masks import make_identity
@@ -22,6 +23,7 @@ Q_BLOCKS = S // P
 HALF = K_PASS // P
 SCALE = HD ** -0.5
 MASKED = -1.0e30
+PIECES = 3
 
 FLOPS = 2 * 2 * B * NH * HD * (K_PASS * K_PASS + K_PASS * S) + 2 * B * S * H * DO
 
@@ -99,6 +101,47 @@ def tile_bloomattention_pa_kernel(tc, q, k, v, w_out, b_out, out):
             base=0,
             channel_multiplier=-1,
         )
+
+        root_left = const.tile([P, PIECES], F32, name="root_left")
+        root = const.tile([P, PIECES], BF16, name="root")
+        by_query = const.tile([P, HALF, P], BF16, name="by_query")
+        by_key = const.tile([P, HALF, P], BF16, name="by_key")
+        far_keys = const.tile([P, BANK], BF16, name="far_keys")
+        far_queries = const.tile([P, BANK], BF16, name="far_queries")
+
+        def make_far_operands():
+            nc.gpsimd.tensor_scalar(
+                out=root_left[:, 0:1], in0=ident_f32[:, 0:1], scalar1=0.0, scalar2=HD ** 0.5, op0=ALU.mult, op1=ALU.add
+            )
+            for r in range(PIECES):
+                nc.gpsimd.tensor_copy(out=root[:, r : r + 1], in_=root_left[:, r : r + 1])
+                if r + 1 < PIECES:
+                    nc.gpsimd.tensor_tensor(
+                        out=root_left[:, r + 1 : r + 2],
+                        in0=root_left[:, r : r + 1],
+                        in1=root[:, r : r + 1],
+                        op=ALU.subtract,
+                    )
+            nc.gpsimd.memset(by_query[:], 0.0)
+            nc.gpsimd.memset(by_key[:], 0.0)
+            query_rows = by_query[:].rearrange("p b (r s) -> p b r s", s=4)[:, :, 0:PIECES, :]
+            key_rows = by_key[:].rearrange("p b (r s) -> p b r s", s=4)[:, :, 0:PIECES, :]
+            pieces = root[:].unsqueeze(1).unsqueeze(3).to_broadcast([P, HALF, PIECES, 2])
+            each = [0, PIECES]
+            small_iota = partial(nc.gpsimd.iota, allow_small_or_imprecise_dtypes=True)
+            small_iota(key_rows[:, :, :, 0], pattern=[[P, HALF], each], base=P - BANK, channel_multiplier=0)
+            small_iota(key_rows[:, :, :, 1], pattern=[[0, HALF], each], base=1 - P, channel_multiplier=1)
+            small_iota(query_rows[:, :, :, 2], pattern=[[-P, HALF], each], base=0, channel_multiplier=0)
+            small_iota(query_rows[:, :, :, 3], pattern=[[0, HALF], each], base=-1, channel_multiplier=-1)
+            nc.gpsimd.tensor_copy(out=query_rows[:, :, :, 0:2], in_=pieces)
+            nc.gpsimd.tensor_copy(out=key_rows[:, :, :, 2:4], in_=pieces)
+
+        def turn_far_operands():
+            for by_position, by_row in ((by_key, far_keys), (by_query, far_queries)):
+                turned = turn_psum.tile([P, BANK], BF16, tag="turn")
+                for blk in range(HALF):
+                    nc.tensor.transpose(turned[:, blk * P : (blk + 1) * P], by_position[:, blk, :], ident_bf[:])
+                nc.vector.tensor_copy(out=by_row[:], in_=turned[:])
 
         e_sets, far_sums = [], []
         for copy in range(2):
@@ -248,8 +291,17 @@ def tile_bloomattention_pa_kernel(tc, q, k, v, w_out, b_out, out):
             head, a = place[unit]
             n = Q_BLOCKS - 1 - a
             far = score_psum.tile([P, BANK], F32, tag="score")
-            scores(far, head, n, 0, HALF)
             banks[unit, 2] = far
+            if head == 0:
+                scores(far, head, n, 0, HALF)
+                return
+            queries = slice(n * P, (n + 1) * P)
+            nc.tensor.matmul(
+                out=far[:], lhsT=q_cols[head][:, queries], rhs=k_cols[head][:, :BANK], start=True, stop=False
+            )
+            nc.tensor.matmul(
+                out=far[:], lhsT=far_queries[:, n * P - BANK : (n + 1) * P - BANK], rhs=far_keys[:], start=False, stop=True
+            )
 
         def maximum_a(unit):
             head, a = place[unit]
@@ -510,6 +562,10 @@ def tile_bloomattention_pa_kernel(tc, q, k, v, w_out, b_out, out):
                         in_=w_out.rearrange("(c p e) n -> p c (e n)", p=P, e=2),
                     )
                     nc.sync.dma_start(out=bias[:], in_=b_out.partition_broadcast(P))
+                if step == -2:
+                    make_far_operands()
+                if step == 1:
+                    turn_far_operands()
                 piece = step - W_STEP
                 if 0 <= piece < W_PIECES:
                     regroup_w(piece)

@@ -496,8 +496,7 @@ def tile_bloomattention_pa_kernel(tc, q, k, v, w_out, b_out, out):
             nc.vector.tensor_tensor(
                 out=results[block][:, n0 : n0 + BANK], in0=products[block, n0][:], in1=bias[:, n0 : n0 + BANK], op=ALU.add
             )
-            if n0 + BANK == DO:
-                nc.sync.dma_start(out=out[b, n * P : (n + 1) * P, :], in_=results[block][:])
+            nc.sync.dma_start(out=out[b, n * P : (n + 1) * P, n0 : n0 + BANK], in_=results[block][:, n0 : n0 + BANK])
 
         project_at = {}
         for b in range(B):
@@ -541,7 +540,7 @@ def tile_bloomattention_pa_kernel(tc, q, k, v, w_out, b_out, out):
                 for_unit(quantise_b, step - 1)
                 for_unit(reciprocals, step - 1)
                 for_unit(quantise_a, step - 1)
-                for_head(quantise_v, step)
+                for_head(quantise_v, step - 1)
                 for_tokens(quantise_c, step - 1)
                 for_unit(near_scores_b, step + 2)
                 for_unit(contexts, step - 2)
@@ -555,7 +554,7 @@ def tile_bloomattention_pa_kernel(tc, q, k, v, w_out, b_out, out):
                 for_unit(normalise, step - 2)
                 for_tokens(turn_c, step)
                 for_head(load_head, step + 10)
-                for_head(regroup_v, step + 6)
+                for_head(regroup_v, step + 4)
                 if step == 0:
                     nc.sync.dma_start(
                         out=w_rows[:].rearrange("p (c e) n -> p c (e n)", e=2),

@@ -36,6 +36,7 @@ W_PIECES = 32
 W_QUARTER = W_PIECES // 4
 PROJECT_LAG = 3
 TURNS = 3
+FAR_HEAD = 2
 PROJECT_EVERY = 4
 
 
@@ -136,11 +137,17 @@ def tile_bloomattention_pa_kernel(tc, q, k, v, w_out, b_out, out):
             nc.gpsimd.tensor_copy(out=query_rows[:, :, :, 0:2], in_=pieces)
             nc.gpsimd.tensor_copy(out=key_rows[:, :, :, 2:4], in_=pieces)
 
+        far_turned = []
+
         def turn_far_operands():
-            for by_position, by_row in ((by_key, far_keys), (by_query, far_queries)):
+            for by_position in (by_key, by_query):
                 turned = turn_psum.tile([P, BANK], BF16, tag="turn")
                 for blk in range(HALF):
                     nc.tensor.transpose(turned[:, blk * P : (blk + 1) * P], by_position[:, blk, :], ident_bf[:])
+                far_turned.append(turned)
+
+        def copy_far_operands():
+            for turned, by_row in zip(far_turned, (far_keys, far_queries)):
                 nc.vector.tensor_copy(out=by_row[:], in_=turned[:])
 
         e_sets, far_sums = [], []
@@ -292,7 +299,7 @@ def tile_bloomattention_pa_kernel(tc, q, k, v, w_out, b_out, out):
             n = Q_BLOCKS - 1 - a
             far = score_psum.tile([P, BANK], F32, tag="score")
             banks[unit, 2] = far
-            if head == 0:
+            if head < FAR_HEAD:
                 scores(far, head, n, 0, HALF)
                 return
             queries = slice(n * P, (n + 1) * P)
@@ -428,7 +435,8 @@ def tile_bloomattention_pa_kernel(tc, q, k, v, w_out, b_out, out):
             if a % 2 == 0:
                 return
             four = slice(a // 2 * HALF, a // 2 * HALF + HALF)
-            nc.gpsimd.tensor_tensor(
+            engine = nc.vector if head < 1 else nc.gpsimd
+            engine.tensor_tensor(
                 out=row_sum[head][:, four], in0=stats[head][:, 3, four], in1=far_sums[head % 2][:, four], op=ALU.add
             )
 
@@ -561,10 +569,12 @@ def tile_bloomattention_pa_kernel(tc, q, k, v, w_out, b_out, out):
                         in_=w_out.rearrange("(c p e) n -> p c (e n)", p=P, e=2),
                     )
                     nc.sync.dma_start(out=bias[:], in_=b_out.partition_broadcast(P))
-                if step == -2:
-                    make_far_operands()
                 if step == 1:
+                    make_far_operands()
+                if step == 4:
                     turn_far_operands()
+                if step == 4:
+                    copy_far_operands()
                 piece = step - W_STEP
                 if 0 <= piece < W_PIECES:
                     regroup_w(piece)

@@ -500,11 +500,25 @@ def tile_bloomattention_pa_kernel(tc, q, k, v, w_out, b_out, out):
             products[block, n0] = product
 
         def add_bias(block, n0):
+            if n0 == 0 or block[0] == B - 1:
+                part = slice(n0, n0 + BANK)
+                nc.vector.tensor_tensor(
+                    out=results[block][:, part], in0=products[block, n0][:], in1=bias[:, part], op=ALU.add
+                )
+                store(block, part)
+
+        def add_bias_beside(block):
+            if block[0] < B - 1:
+                part = slice(BANK, DO)
+                nc.scalar.copy(out=results[block][:, part], in_=products[block, BANK][:])
+                nc.gpsimd.tensor_tensor(
+                    out=results[block][:, part], in0=results[block][:, part], in1=bias[:, part], op=ALU.add
+                )
+                store(block, part)
+
+        def store(block, part):
             b, n = block
-            nc.vector.tensor_tensor(
-                out=results[block][:, n0 : n0 + BANK], in0=products[block, n0][:], in1=bias[:, n0 : n0 + BANK], op=ALU.add
-            )
-            nc.sync.dma_start(out=out[b, n * P : (n + 1) * P, n0 : n0 + BANK], in_=results[block][:, n0 : n0 + BANK])
+            nc.sync.dma_start(out=out[b, n * P : (n + 1) * P, part], in_=results[block][:, part])
 
         project_at = {}
         for b in range(B):
@@ -538,6 +552,7 @@ def tile_bloomattention_pa_kernel(tc, q, k, v, w_out, b_out, out):
                 for_unit(exponential_far, step)
                 for_unit(turn_b, step)
                 for_unit(exponential_a, step)
+                for_tokens(add_bias_beside, step - 3)
                 for_unit(gather_a, step - 1)
                 for_head(copy_k, step + 3)
                 for_tokens(gather_c, step - 1)

from contextlib import ExitStack
from functools import partial

import concourse.mybir as mybir
from concourse.masks import make_identity

BF16 = mybir.dt.bfloat16
F32 = mybir.dt.float32
I32 = mybir.dt.int32
U32 = mybir.dt.uint32
U8 = mybir.dt.uint8
FP8X4 = mybir.dt.float8_e4m3fn_x4
ALU = mybir.AluOpType
ACT = mybir.ActivationFunctionType
ROW = mybir.AxisListType.X

B, NH, S, HD, DO = 2, 8, 1024, 128, 1024
H = NH * HD
P = 128
BANK = 512
K_PASS = 512
Q_BLOCKS = S // P
HALF = K_PASS // P
SCALE = HD ** -0.5
MASKED = -1.0e30
PIECES = 3

FLOPS = 2 * 2 * B * NH * HD * (K_PASS * K_PASS + K_PASS * S) + 2 * B * S * H * DO

HEADS = B * NH
UNITS = Q_BLOCKS // 2

LOAD_LEAD = 10
W_STEP = 1
W_PIECES = 32
W_QUARTER = W_PIECES // 4
PROJECT_LAG = 3
TURNS = 3
FAR_HEAD = 2
PROJECT_EVERY = 4


def regroup(nc, rows, grouped):
    nc.gpsimd.tensor_scalar(
        out=grouped,
        in0=rows.rearrange("p (g t) w -> p g w t", t=4),
        scalar1=1.0,
        scalar2=0.0,
        op0=ALU.mult,
        op1=ALU.add,
    )


def turn_words(nc, turned, rows, n_pass, ident_f32):
    words = rows.bitcast(F32)
    for piece in range(2 * n_pass):
        nc.tensor.transpose(turned[:, piece, :], words[:, piece * P : (piece + 1) * P], ident_f32)


def gather_words(nc, grouped, turned):
    nc.scalar.copy(out=grouped, in_=turned.rearrange("p (g u) r -> p g r u", u=2))


def quantise_words(nc, pool, grouped, n, tag):
    codes = pool.tile([P, n * P], U32, tag=tag + "_codes%d" % n, align_bytes=64)
    scales = pool.tile([P, n * P], U8, tag=tag + "_scales%d" % n, align_bytes=64)
    nc.vector.quantize_mx(
        out=codes[:].bitcast(FP8X4),
        scales=scales[:],
        in_=grouped[:].rearrange("p g r u -> p (g r u)").bitcast(BF16),
    )
    return codes, scales


def tile_bloomattention_pa_kernel(tc, q, k, v, w_out, b_out, out):
    nc = tc.nc
    with ExitStack() as ctx:
        const = ctx.enter_context(tc.tile_pool(name="const", bufs=1))
        loads = ctx.enter_context(tc.tile_pool(name="loads", bufs=3))
        heads = ctx.enter_context(tc.tile_pool(name="heads", bufs=3))
        blocks = ctx.enter_context(tc.tile_pool(name="blocks", bufs=3))
        score_psum = ctx.enter_context(tc.psum_pool(name="score_psum", bufs=5))
        turn_psum = ctx.enter_context(tc.psum_pool(name="turn_psum", bufs=3))

        ident_bf = const.tile([P, P], BF16, name="ident_bf")
        make_identity(nc, ident_bf[:])
        ident_f32 = const.tile([P, P], F32, name="ident_f32")
        make_identity(nc, ident_f32[:])

        distance = const.tile([P, S], I32, name="distance")
        nc.gpsimd.iota(distance[:], pattern=[[1, S]], base=0, channel_multiplier=-1)
        penalty = const.tile([P, S], F32, name="penalty")
        nc.vector.tensor_scalar(
            out=penalty[:], in0=distance[:], scalar1=-(HD ** 0.5), scalar2=None, op0=ALU.mult
        )
        nc.gpsimd.affine_select(
            out=penalty[:, :P],
            in_=penalty[:, :P],
            pattern=[[1, P]],
            compare_op=ALU.is_ge,
            fill=MASKED,
            base=0,
            channel_multiplier=-1,
        )

        root_left = const.tile([P, PIECES], F32, name="root_left")
        root = const.tile([P, PIECES], BF16, name="root")
        by_query = const.tile([P, HALF, P], BF16, name="by_query")
        by_key = const.tile([P, HALF, P], BF16, name="by_key")
        far_keys = const.tile([P, BANK], BF16, name="far_keys")
        far_queries = const.tile([P, BANK], BF16, name="far_queries")

        def make_far_operands():
            nc.gpsimd.tensor_scalar(
                out=root_left[:, 0:1], in0=ident_f32[:, 0:1], scalar1=0.0, scalar2=HD ** 0.5, op0=ALU.mult, op1=ALU.add
            )
            for r in range(PIECES):
                nc.gpsimd.tensor_copy(out=root[:, r : r + 1], in_=root_left[:, r : r + 1])
                if r + 1 < PIECES:
                    nc.gpsimd.tensor_tensor(
                        out=root_left[:, r + 1 : r + 2],
                        in0=root_left[:, r : r + 1],
                        in1=root[:, r : r + 1],
                        op=ALU.subtract,
                    )
            nc.gpsimd.memset(by_query[:], 0.0)
            nc.gpsimd.memset(by_key[:], 0.0)
            query_rows = by_query[:].rearrange("p b (r s) -> p b r s", s=4)[:, :, 0:PIECES, :]
            key_rows = by_key[:].rearrange("p b (r s) -> p b r s", s=4)[:, :, 0:PIECES, :]
            pieces = root[:].unsqueeze(1).unsqueeze(3).to_broadcast([P, HALF, PIECES, 2])
            each = [0, PIECES]
            small_iota = partial(nc.gpsimd.iota, allow_small_or_imprecise_dtypes=True)
            small_iota(key_rows[:, :, :, 0], pattern=[[P, HALF], each], base=P - BANK, channel_multiplier=0)
            small_iota(key_rows[:, :, :, 1], pattern=[[0, HALF], each], base=1 - P, channel_multiplier=1)
            small_iota(query_rows[:, :, :, 2], pattern=[[-P, HALF], each], base=0, channel_multiplier=0)
            small_iota(query_rows[:, :, :, 3], pattern=[[0, HALF], each], base=-1, channel_multiplier=-1)
            nc.gpsimd.tensor_copy(out=query_rows[:, :, :, 0:2], in_=pieces)
            nc.gpsimd.tensor_copy(out=key_rows[:, :, :, 2:4], in_=pieces)

        far_turned = []

        def turn_far_operands():
            for by_position in (by_key, by_query):
                turned = turn_psum.tile([P, BANK], BF16, tag="turn")
                for blk in range(HALF):
                    nc.tensor.transpose(turned[:, blk * P : (blk + 1) * P], by_position[:, blk, :], ident_bf[:])
                far_turned.append(turned)

        def copy_far_operands():
            for turned, by_row in zip(far_turned, (far_keys, far_queries)):
                nc.vector.tensor_copy(out=by_row[:], in_=turned[:])

        e_sets, far_sums = [], []
        for copy in range(2):
            e_tiles = []
            for n in range(Q_BLOCKS):
                e_tile = const.tile([P, K_PASS * (n // HALF + 1)], BF16, name="e%d_%d" % (copy, n))
                if (n + 1) % HALF != 0:
                    nc.vector.memset(e_tile[:, P * (n + 1) :], 0.0)
                e_tiles.append(e_tile)
            e_sets.append(e_tiles)
            far_sum = const.tile([P, Q_BLOCKS], F32, name="far_sum%d" % copy)
            nc.vector.memset(far_sum[:], 0.0)
            far_sums.append(far_sum)

        w_rows = const.tile([P, H // P, DO], BF16, name="w_rows")
        w_grouped = const.tile([P, H // K_PASS, DO, 4], BF16, name="w_grouped", align_bytes=64)
        w_codes = const.tile([P, H // K_PASS, DO], U32, name="w_codes", align_bytes=64)
        w_scales = const.tile([P, H // K_PASS, DO], U8, name="w_scales", align_bytes=64)
        bias = const.tile([P, DO], BF16, name="bias")

        q_rows, k_rows, v_rows, turned_rows, q_cols, k_cols = {}, {}, {}, {}, {}, {}
        v_grouped, v_codes, v_scales = {}, {}, {}
        stats, row_scale, row_sum = {}, {}, {}
        c_rows, context = {}, {}
        banks, e_turned, e_grouped, e_codes, e_scales = {}, {}, {}, {}, {}
        c_turned, c_grouped, c_codes, c_scales, products, results = {}, {}, {}, {}, {}, {}

        def load_head(head):
            b, h = divmod(head, NH)
            q_tile = loads.tile([P, Q_BLOCKS, HD], BF16, tag="q_rows")
            nc.sync.dma_start(out=q_tile[:], in_=q[b, h].rearrange("(n p) d -> p n d", p=P))
            k_tile = loads.tile([P, Q_BLOCKS, HD], BF16, tag="k_rows")
            nc.sync.dma_start(out=k_tile[:], in_=k[b, h].rearrange("(n p) d -> p n d", p=P))
            v_tile = loads.tile([P, S // P, HD], BF16, tag="v_rows")
            nc.sync.dma_start(
                out=v_tile[:].rearrange("p (c e) d -> p c (e d)", e=2),
                in_=v[b, h].rearrange("(c p e) d -> p c (e d)", p=P, e=2),
            )
            q_rows[head], k_rows[head], v_rows[head] = q_tile, k_tile, v_tile

        def turn_rows(rows, tag):
            turned = turn_psum.tile([P, S], BF16, tag="turn")
            for n in range(Q_BLOCKS):
                nc.tensor.transpose(turned[:, n * P : (n + 1) * P], rows[:, n, :], ident_bf[:])
            turned_rows[tag] = turned

        def slope(head):
            return 2.0 ** -(head % NH + 1)

        def turn_q(head):
            turn_rows(q_rows[head], "q_cols")

        def copy_q(head):
            columns = heads.tile([P, S], BF16, tag="q_cols")
            nc.vector.tensor_scalar(
                out=columns[:], in0=turned_rows["q_cols"][:], scalar1=1.0 / slope(head), scalar2=None, op0=ALU.mult
            )
            q_cols[head] = columns

        def turn_k(head):
            turn_rows(k_rows[head], "k_cols")

        def copy_k(head):
            columns = heads.tile([P, S], BF16, tag="k_cols")
            nc.scalar.copy(out=columns[:], in_=turned_rows["k_cols"][:])
            k_cols[head] = columns

        def regroup_v(head):
            grouped = heads.tile([P, S // K_PASS, HD, 4], BF16, tag="v_grouped", align_bytes=64)
            for g in range(S // K_PASS):
                for d in range(0, HD, HD // 2):
                    columns = slice(d, d + HD // 2)
                    regroup(nc, v_rows[head][:, 4 * g : 4 * g + 4, columns], grouped[:, g : g + 1, columns, :])
            v_grouped[head] = grouped

        def quantise_v(head):
            codes = heads.tile([P, S // K_PASS, HD], U32, tag="v_codes", align_bytes=64)
            scales = heads.tile([P, S // K_PASS, HD], U8, tag="v_scales", align_bytes=64)
            nc.vector.quantize_mx(
                out=codes[:].rearrange("p g d -> p (g d)").bitcast(FP8X4),
                scales=scales[:].rearrange("p g d -> p (g d)"),
                in_=v_grouped[head][:].rearrange("p g d t -> p (g d t)"),
            )
            v_codes[head], v_scales[head] = codes, scales

        def regroup_w(piece):
            g, part = divmod(piece, W_PIECES // 2)
            width = DO // (W_PIECES // 2)
            columns = slice(part * width, (part + 1) * width)
            regroup(nc, w_rows[:, 4 * g : 4 * g + 4, columns], w_grouped[:, g : g + 1, columns, :])

        def quantise_w(quarter):
            g, part = divmod(quarter, DO // BANK)
            columns = slice(part * BANK, (part + 1) * BANK)
            nc.vector.quantize_mx(
                out=w_codes[:, g, columns].bitcast(FP8X4),
                scales=w_scales[:, g, columns],
                in_=w_grouped[:, g, columns, :].rearrange("p n t -> p (n t)"),
            )

        place = [(head, a) for head in range(HEADS - TURNS) for a in range(UNITS)]
        for first in range(0, UNITS, 2):
            place += [(head, a) for head in range(HEADS - TURNS, HEADS) for a in range(first, first + 2)]
        first_unit = [place.index((head, 0)) for head in range(HEADS)]

        def column(n):
            return (0, 1, HALF, HALF + 1, HALF + 2, HALF + 3, 2, 3)[n]

        def scores(bank, head, n, first, count):
            for blk in range(count):
                back = n - first - blk
                nc.tensor.matmul(
                    out=bank[:, blk * P : (blk + 1) * P],
                    lhsT=penalty[:, back * P : (back + 1) * P],
                    rhs=ident_f32[:],
                    start=(blk == 0),
                    stop=False,
                    is_transpose=True,
                )
            nc.tensor.matmul(
                out=bank[:, : count * P],
                lhsT=q_cols[head][:, n * P : (n + 1) * P],
                rhs=k_cols[head][:, first * P : (first + count) * P],
                start=False,
                stop=True,
            )

        def near_scores(unit, far):
            head, a = place[unit]
            n = Q_BLOCKS - 1 - a if far else a
            if far and a == 0:
                tile = heads.tile([P, 4, Q_BLOCKS], F32, tag="stats")
                factors = heads.tile([P, Q_BLOCKS], F32, tag="row_scale")
                sums = heads.tile([P, Q_BLOCKS], F32, tag="row_sum")
                stats[head], row_scale[head], row_sum[head] = tile, factors, sums
            near = score_psum.tile([P, BANK], F32, tag="score")
            scores(near, head, n, n // HALF * HALF, n % HALF + 1)
            banks[unit, far] = near

        def near_scores_a(unit):
            near_scores(unit, 0)

        def near_scores_b(unit):
            near_scores(unit, 1)

        def far_scores(unit):
            head, a = place[unit]
            n = Q_BLOCKS - 1 - a
            far = score_psum.tile([P, BANK], F32, tag="score")
            banks[unit, 2] = far
            if head < FAR_HEAD:
                scores(far, head, n, 0, HALF)
                return
            queries = slice(n * P, (n + 1) * P)
            nc.tensor.matmul(
                out=far[:], lhsT=q_cols[head][:, queries], rhs=k_cols[head][:, :BANK], start=True, stop=False
            )
            nc.tensor.matmul(
                out=far[:], lhsT=far_queries[:, n * P - BANK : (n + 1) * P - BANK], rhs=far_keys[:], start=False, stop=True
            )

        def maximum_a(unit):
            head, a = place[unit]
            nc.vector.tensor_reduce(
                out=stats[head][:, 0, column(a) : column(a) + 1], in_=banks[unit, 0][:, : (a + 1) * P], axis=ROW, op=ALU.max
            )

        def shift_a(unit):
            head, a = place[unit]
            nc.scalar.activation(
                out=stats[head][:, 2, column(a) : column(a) + 1], in_=stats[head][:, 0, column(a) : column(a) + 1], func=ACT.Copy, scale=-SCALE * slope(head)
            )

        def maximum_b(unit):
            head, a = place[unit]
            n = Q_BLOCKS - 1 - a
            nc.vector.tensor_reduce(
                out=stats[head][:, 0, column(n) : column(n) + 1], in_=banks[unit, 1][:, : (HALF - a) * P], axis=ROW, op=ALU.max
            )

        def maximum_far(unit):
            head, a = place[unit]
            n = Q_BLOCKS - 1 - a
            nc.vector.tensor_reduce(out=stats[head][:, 1, column(n) : column(n) + 1], in_=banks[unit, 2][:], axis=ROW, op=ALU.max)

        def shift_b(unit):
            head, a = place[unit]
            n = Q_BLOCKS - 1 - a
            nc.vector.tensor_scalar(
                out=stats[head][:, 2, column(n) : column(n) + 1],
                in0=stats[head][:, 0, column(n) : column(n) + 1],
                scalar1=stats[head][:, 1, column(n) : column(n) + 1],
                scalar2=-SCALE * slope(head),
                op0=ALU.max,
                op1=ALU.mult,
            )

        def exponential(unit, n, bank, first, width, sums):
            head = place[unit][0]
            nc.scalar.activation(
                out=e_sets[head % 2][n][:, first : first + width],
                in_=bank[:, :width],
                func=ACT.Exp,
                bias=stats[head][:, 2, column(n) : column(n) + 1],
                scale=SCALE * slope(head),
                accum_out=sums[:, column(n) : column(n) + 1],
            )

        def exponential_a(unit):
            head, a = place[unit]
            exponential(unit, a, banks[unit, 0], 0, (a + 1) * P, stats[head][:, 3, :])

        def exponential_b(unit):
            head, a = place[unit]
            exponential(unit, Q_BLOCKS - 1 - a, banks[unit, 1], BANK, (HALF - a) * P, stats[head][:, 3, :])

        def exponential_far(unit):
            head, a = place[unit]
            n = Q_BLOCKS - 1 - a
            exponential(unit, n, banks[unit, 2], 0, BANK, far_sums[head % 2])

        def turn_a(unit):
            head, a = place[unit]
            if a % 2 == 1:
                turned = turn_psum.tile([P, HALF, P], F32, tag="turn")
                e_turned[unit // 2, 0] = turned
                for m in range(2):
                    turn_words(nc, turned[:, 2 * m : 2 * m + 2, :], e_sets[head % 2][a - 1 + m][:], 1, ident_f32[:])

        def turn_b(unit):
            head, a = place[unit]
            turned = turn_psum.tile([P, HALF, P], F32, tag="turn")
            e_turned[unit, 1] = turned
            turn_words(nc, turned[:], e_sets[head % 2][Q_BLOCKS - 1 - a][:], 2, ident_f32[:])

        def gather_a(unit):
            if unit % 2 == 1:
                pair = blocks.tile([P, 2, P, 2], F32, tag="e_grouped_a", align_bytes=64)
                e_grouped[unit // 2, 0] = pair
                gather_words(nc, pair[:], e_turned[unit // 2, 0][:])

        def gather_b(unit):
            if unit % 2 == 0:
                pair = blocks.tile([P, 4, P, 2], F32, tag="e_grouped_b", align_bytes=64)
                e_grouped[unit // 2, 1] = pair
            first = 2 - 2 * (unit % 2)
            gather_words(nc, e_grouped[unit // 2, 1][:, first : first + 2, :, :], e_turned[unit, 1][:])

        def quantise_a(unit):
            if unit % 2 == 1:
                e_codes[unit // 2, 0], e_scales[unit // 2, 0] = quantise_words(nc, blocks, e_grouped[unit // 2, 0], 2, "e_a")

        def quantise_b(unit):
            if unit % 2 == 1:
                e_codes[unit // 2, 1], e_scales[unit // 2, 1] = quantise_words(nc, blocks, e_grouped[unit // 2, 1], 4, "e_b")

        def half_rows(tile, half):
            pairs = tile.rearrange("p (x y) d -> p x y d", y=2)
            return pairs[:, 1:3] if half else pairs[:, 0::3]

        def contexts(unit):
            head, a = place[unit]
            if a % 2 == 0:
                return
            half = unit // 2
            bank = turn_psum.tile([P, HALF, HD], F32, tag="turn")
            context[half] = bank
            for m in range(HALF):
                part, n_pass = m // 2, m // 2 + 1
                for g in range(n_pass):
                    first = (m % 2 * n_pass + g) * P
                    nc.tensor.matmul_mx(
                        out=bank[:, m, :],
                        lhsT=e_codes[half, part][:, first : first + P].bitcast(FP8X4),
                        lhsT_scale=e_scales[half, part][:, first : first + P],
                        rhs=v_codes[head][:, g, :].bitcast(FP8X4),
                        rhs_scale=v_scales[head][:, g, :],
                        start=(g == 0),
                        stop=(g == n_pass - 1),
                    )

        def row_sums(unit):
            head, a = place[unit]
            if a % 2 == 0:
                return
            four = slice(a // 2 * HALF, a // 2 * HALF + HALF)
            engine = nc.vector if head < 1 else nc.gpsimd
            engine.tensor_tensor(
                out=row_sum[head][:, four], in0=stats[head][:, 3, four], in1=far_sums[head % 2][:, four], op=ALU.add
            )

        def reciprocals(unit):
            head, a = place[unit]
            if a % 2 == 0:
                return
            four = slice(a // 2 * HALF, a // 2 * HALF + HALF)
            nc.vector.reciprocal(out=row_scale[head][:, four], in_=row_sum[head][:, four])

        def normalise(unit):
            head, a = place[unit]
            b, h = divmod(head, NH)
            if a % 2 == 0:
                return
            if h == 0 and a == 1:
                rows = heads.tile([P, Q_BLOCKS, H], BF16, tag="c_rows", bufs=2)
                c_rows[b] = rows
            factors = row_scale[head][:, a // 2 * HALF : a // 2 * HALF + HALF]
            nc.vector.tensor_tensor(
                out=half_rows(c_rows[b][:, :, h * HD : (h + 1) * HD], a // 2),
                in0=context[unit // 2][:].rearrange("p (x y) d -> p x y d", y=2),
                in1=factors.rearrange("p (x y) -> p x y", y=2).unsqueeze(3).to_broadcast([P, 2, 2, HD]),
                op=ALU.mult,
            )

        def turn_c(block):
            b, n = block
            turned = turn_psum.tile([P, HALF, P], F32, tag="turn")
            turn_words(nc, turned[:], c_rows[b][:, n, :], H // K_PASS, ident_f32[:])
            c_turned[block] = turned

        def gather_c(block):
            grouped = blocks.tile([P, H // K_PASS, P, 2], F32, tag="c_grouped", align_bytes=64)
            gather_words(nc, grouped[:], c_turned[block][:])
            c_grouped[block] = grouped

        def quantise_c(block):
            c_codes[block], c_scales[block] = quantise_words(nc, blocks, c_grouped[block], H // K_PASS, "c")

        def project(block, n0):
            b, n = block
            if n0 == 0:
                result = blocks.tile([P, DO], F32, tag="result", bufs=5)
                results[block] = result
            if True:
                if b == B - 1:
                    product = score_psum.tile([P, BANK], F32, tag="score")
                else:
                    product = turn_psum.tile([P, BANK], F32, tag="turn")
                for g in range(H // K_PASS):
                    nc.tensor.matmul_mx(
                        out=product[:],
                        lhsT=c_codes[block][:, g * P : (g + 1) * P].bitcast(FP8X4),
                        lhsT_scale=c_scales[block][:, g * P : (g + 1) * P],
                        rhs=w_codes[:, g, n0 : n0 + BANK].bitcast(FP8X4),
                        rhs_scale=w_scales[:, g, n0 : n0 + BANK],
                        start=(g == 0),
                        stop=(g == H // K_PASS - 1),
                    )
            products[block, n0] = product

        def add_bias(block, n0):
            if n0 == 0 or block[0] == B - 1:
                part = slice(n0, n0 + BANK)
                nc.vector.tensor_tensor(
                    out=results[block][:, part], in0=products[block, n0][:], in1=bias[:, part], op=ALU.add
                )
                store(block, part)

        def add_bias_beside(block):
            if block[0] < B - 1:
                part = slice(BANK, DO)
                nc.scalar.copy(out=results[block][:, part], in_=products[block, BANK][:])
                nc.gpsimd.tensor_tensor(
                    out=results[block][:, part], in0=results[block][:, part], in1=bias[:, part], op=ALU.add
                )
                store(block, part)

        def store(block, part):
            b, n = block
            nc.sync.dma_start(out=out[b, n * P : (n + 1) * P, part], in_=results[block][:, part])

        project_at = {}
        for b in range(B):
            for half in range(2):
                for m, n in enumerate(((0, 1, 6, 7), (2, 3, 4, 5))[half]):
                    ready = place.index((b * NH + NH - 1, 2 * half + 1)) + PROJECT_LAG
                    project_at[b, n] = ready + PROJECT_EVERY * (HALF * half + m) if b + 1 < B else ready + m

        def for_unit(stage, unit):
            if 0 <= unit < len(place):
                stage(unit)

        def for_head(prepare, step):
            if step in first_unit:
                prepare(first_unit.index(step))

        def for_tokens(stage, step, *columns):
            for block in project_at:
                if project_at[block] == step:
                    stage(block, *columns)

        with tc.manual_schedule():
            for step in range(-LOAD_LEAD, HEADS * UNITS + PROJECT_LAG + 8):
                for_tokens(add_bias, step - 3, 0)
                for_tokens(add_bias, step - 3, BANK)
                for_unit(maximum_b, step + 1)
                for_unit(shift_a, step)
                for_unit(exponential_b, step)
                for_unit(maximum_far, step + 1)
                for_unit(near_scores_a, step + 1)
                for_unit(exponential_far, step)
                for_unit(turn_b, step)
                for_unit(exponential_a, step)
                for_tokens(add_bias_beside, step - 3)
                for_unit(gather_a, step - 1)
                for_head(copy_k, step + 3)
                for_tokens(gather_c, step - 1)
                for_unit(maximum_a, step + 1)
                for_unit(row_sums, step - 1)
                for_unit(shift_b, step + 1)
                for_head(copy_q, step + 5)
                for_unit(quantise_b, step - 1)
                for_unit(reciprocals, step - 1)
                for_unit(quantise_a, step - 1)
                for_head(quantise_v, step - 1)
                for_tokens(quantise_c, step - 1)
                for_unit(near_scores_b, step + 2)
                for_unit(contexts, step - 2)
                for_tokens(project, step - 2, 0)
                for_tokens(project, step - 2, BANK)
                for_unit(far_scores, step + 2)
                for_unit(turn_a, step)
                for_unit(gather_b, step)
                for_head(turn_k, step + 4)
                for_head(turn_q, step + 6)
                for_unit(normalise, step - 2)
                for_tokens(turn_c, step)
                for_head(load_head, step + 10)
                for_head(regroup_v, step + 4)
                if step == 0:
                    nc.sync.dma_start(
                        out=w_rows[:].rearrange("p (c e) n -> p c (e n)", e=2),
                        in_=w_out.rearrange("(c p e) n -> p c (e n)", p=P, e=2),
                    )
                    nc.sync.dma_start(out=bias[:], in_=b_out.partition_broadcast(P))
                if step == 1:
                    make_far_operands()
                if step == 4:
                    turn_far_operands()
                if step == 4:
                    copy_far_operands()
                piece = step - W_STEP
                if 0 <= piece < W_PIECES:
                    regroup_w(piece)
                if piece > 0 and piece % W_QUARTER == 0 and piece <= W_PIECES:
                    quantise_w(piece // W_QUARTER - 1)
